import numpy as np
import ml_dtypes


def mxq(x, axis, fmt="e4m3"):
    dtype, down = {"e4m3": (ml_dtypes.float8_e4m3fn, 7), "e5m2": (ml_dtypes.float8_e5m2, 14)}[fmt]
    v = np.moveaxis(np.asarray(x, np.float32).astype(ml_dtypes.bfloat16).astype(np.float64), axis, -1)
    blocks = v.reshape(v.shape[:-1] + (-1, 32))
    amax = np.abs(blocks).max(-1, keepdims=True)
    byte = np.maximum(np.where(amax > 0, np.frexp(amax)[1] - 1 + 127, 0) - down, 1)
    scale = np.exp2(byte - 127.0)
    codes = (blocks / scale).astype(np.float32).astype(dtype).astype(np.float64)
    return np.moveaxis((codes * scale).reshape(v.shape), -1, axis)


WIDE = False


def mx_kscale(k):
    if not WIDE:
        return np.ones(k)
    levels = np.array([10, -10, 5, -5, 0])
    if k % 512:
        return np.exp2(np.random.permutation(np.resize(levels, k // 32))).repeat(32)
    a = np.empty((k // 512, 16))
    for p in range(k // 512):
        a[p, :8] = np.random.permutation(np.resize(levels, 8))
        for g in range(8):
            far = levels[np.abs(levels - a[p, g]) >= 10]
            a[p, g + 8] = far[np.random.randint(len(far))]
    return np.exp2(a.ravel()).repeat(32)


BF16 = ml_dtypes.bfloat16


def bf(x):
    return np.asarray(x, np.float32).astype(BF16)


def f64(x):
    return np.asarray(x).astype(np.float64)


B, T, D, K, CD, CF, M = 8, 16, 1024, 4, 128, 512, 256
LN_EPS = 1e-5


def setup_inputs():
    s = mx_kscale(D)
    t = mx_kscale(CF)
    return {
        "h": bf(np.random.standard_normal((B, T, D)) * s),
        "mu_w1_h": bf(np.random.standard_normal((D, CF)) / np.sqrt(D) / s[:, None]),
        "code_mu": bf(np.random.standard_normal((K, CF)) * 0.4),
        "mu_b1": bf(np.random.standard_normal(CF) * 0.2),
        "ln_g": bf((1.0 + 0.1 * np.random.standard_normal(CF)) * t),
        "ln_b": bf(np.random.standard_normal(CF) * 0.2 * t),
        "mu_w2": bf(np.random.standard_normal((CF, CF)) / np.sqrt(CF) / t[:, None]),
        "mu_b2": bf(np.random.standard_normal(CF) * 0.2),
    }


def reference(h, mu_w1_h, code_mu, mu_b1, ln_g, ln_b, mu_w2, mu_b2):
    hp = mxq(f64(h), 2, "e4m3") @ mxq(f64(mu_w1_h), 0, "e4m3")
    mu_pre = hp[:, :, None, :] + f64(code_mu) + f64(mu_b1)
    mean = mu_pre.mean(-1, keepdims=True)
    var = np.square(mu_pre - mean).mean(-1, keepdims=True)
    mu_ln = (mu_pre - mean) * (1.0 / np.sqrt(var + LN_EPS)) * f64(ln_g) + f64(ln_b)
    return np.tanh((mxq(mu_ln, 3, "e4m3") @ mxq(f64(mu_w2), 0, "e4m3")) + f64(mu_b2))

@@ -1,0 +1,240 @@
+from contextlib import ExitStack
+
+import concourse.mybir as mybir
+from concourse.masks import make_identity
+
+F32 = mybir.dt.float32
+BF16 = mybir.dt.bfloat16
+U32 = mybir.dt.uint32
+U8 = mybir.dt.uint8
+FP8X4 = mybir.dt.float8_e4m3fn_x4
+ALU = mybir.AluOpType
+ACT = mybir.ActivationFunctionType
+
+P = 128
+PACK = 4
+D = 1024
+PASSES1 = D // (P * PACK)
+CODES = 4
+CF = 512
+LN_EPS = 1e-5
+
+ROW_G, ROW_B, ROW_B2, ROW_B1 = 4, 5, 6, 7
+VECTORS = 8
+
+QUANTISE_LAG = 2
+FINISH_LAG = 3
+
+FLOPS = 2 * P * D * CF + 2 * P * CODES * CF * CF
+
+
+def regroup(copy, grouped, rows):
+    copy(
+        out=grouped.rearrange("p (c i) j -> p c j i", i=4),
+        in_=rows.rearrange("p j (c i) -> p c j i", i=4),
+    )
+
+
+def tile_mixtureconfounderprior_pa_s_kernel(
+    tc, h, mu_w1_h, code_mu, mu_b1, ln_g, ln_b, mu_w2, mu_b2, out
+):
+    nc = tc.nc
+    h_rows = h.flatten_outer_dims()
+    out_rows = out.rearrange("b t k n -> (b t) k n")
+
+    with ExitStack() as stack:
+        keep = stack.enter_context(tc.tile_pool(name="keep", bufs=1))
+        psum_once = stack.enter_context(tc.psum_pool(name="psum_once", bufs=1))
+        psum_turn = stack.enter_context(tc.psum_pool(name="psum_turn", bufs=3))
+        psum_out = stack.enter_context(tc.psum_pool(name="psum_out", bufs=2))
+        stack.enter_context(tc.manual_schedule())
+
+        vec_rows = keep.tile([P, CF], BF16)
+        nc.vector.memset(vec_rows[:], 0.0)
+        nc.sync.dma_start(out=vec_rows[0:CODES, :], in_=code_mu)
+        for row, vector in ((ROW_B1, mu_b1), (ROW_G, ln_g), (ROW_B, ln_b), (ROW_B2, mu_b2)):
+            nc.sync.dma_start(out=vec_rows[row : row + 1, :], in_=vector.unsqueeze(0))
+
+        h_sb = keep.tile([P, D], BF16)
+        nc.sync.dma_start(out=h_sb[:], in_=h_rows)
+        w1_rows = keep.tile([P, PASSES1, PACK, CF], BF16)
+        w1_view = mu_w1_h.rearrange("(g p j) n -> g p j n", g=PASSES1, j=PACK)
+        for g in range(PASSES1):
+            nc.sync.dma_start(out=w1_rows[:, g], in_=w1_view[g])
+        w2_rows = keep.tile([P, PACK, CF], BF16)
+        nc.sync.dma_start(out=w2_rows[:], in_=mu_w2.rearrange("(p j) n -> p j n", j=PACK))
+
+        ident_bf16 = keep.tile([P, P], BF16)
+        make_identity(nc, ident_bf16[:])
+        ident_f32 = keep.tile([P, P], F32)
+        make_identity(nc, ident_f32[:])
+        eps = keep.tile([P, 1], F32)
+        nc.vector.memset(eps[:], LN_EPS)
+        table_warm = keep.tile([P, 2], F32)
+        nc.scalar.activation(out=table_warm[:, 0:1], in_=eps[:], func=ACT.Sqrt)
+
+        cols_ps = psum_turn.tile([P, PACK, P], BF16, tag="turn")
+        for c in range(PACK):
+            nc.tensor.transpose(cols_ps[:, c, :], vec_rows[:, c * P : (c + 1) * P], ident_bf16[:])
+        vec_cols = keep.tile([P, PACK, VECTORS], F32)
+        nc.vector.tensor_copy(out=vec_cols[:], in_=cols_ps[:, :, 0:VECTORS])
+        nc.vector.tensor_tensor(
+            out=vec_cols[:, :, 0:CODES],
+            in0=vec_cols[:, :, 0:CODES],
+            in1=vec_cols[:, :, ROW_B1 : ROW_B1 + 1].to_broadcast([P, PACK, CODES]),
+            op=ALU.add,
+        )
+
+        h_words = h_sb[:].bitcast(F32)
+        hT_ps = psum_turn.tile([P, PASSES1, 2, P], F32, tag="turn")
+        for g in range(PASSES1):
+            for u in range(2):
+                words = slice(2 * P * g + u, 2 * P * (g + 1), 2)
+                nc.tensor.transpose(hT_ps[:, g, u, :], h_words[:, words], ident_f32[:])
+        h_grouped = keep.tile([P, PASSES1 * P * PACK], BF16, align_bytes=64)
+        nc.scalar.copy(
+            out=h_grouped[:].bitcast(F32).rearrange("p (g t u) -> p g t u", g=PASSES1, u=2),
+            in_=hT_ps[:].rearrange("p g u t -> p g t u"),
+        )
+
+        def spread(all_ps, j):
+            for c in range(PACK):
+                nc.tensor.transpose(
+                    all_ps[:, c * P : (c + 1) * P],
+                    vec_cols[:, c, j : j + 1].to_broadcast([P, P]),
+                    ident_f32[:],
+                )
+
+        c_all = keep.tile([P, CODES, CF], F32)
+        for k in range(CODES):
+            c_ps = psum_turn.tile([P, CF], F32, tag="turn")
+            spread(c_ps, k)
+            nc.scalar.copy(out=c_all[:, k, :], in_=c_ps[:])
+
+        h_codes = keep.tile([P, PASSES1 * P], U32, align_bytes=64)
+        h_scales = keep.tile([P, PASSES1 * P], U8, align_bytes=64)
+        w1_grouped = keep.tile([P, PASSES1, CF, PACK], BF16, align_bytes=64)
+        w1_codes = keep.tile([P, PASSES1, CF], U32, align_bytes=64)
+        w1_scales = keep.tile([P, PASSES1, CF], U8, align_bytes=64)
+        regroup(nc.vector.tensor_copy, w1_grouped[:, 0], w1_rows[:, 0])
+        nc.vector.quantize_mx(out=h_codes[:].bitcast(FP8X4), scales=h_scales[:], in_=h_grouped[:])
+        regroup(nc.vector.tensor_copy, w1_grouped[:, 1], w1_rows[:, 1])
+        for g in range(PASSES1):
+            nc.vector.quantize_mx(
+                out=w1_codes[:, g, :].bitcast(FP8X4),
+                scales=w1_scales[:, g, :],
+                in_=w1_grouped[:, g].rearrange("p n j -> p (n j)"),
+            )
+
+        hp_ps = psum_once.tile([P, CF], F32)
+        for g in range(PASSES1):
+            nc.tensor.matmul_mx(
+                out=hp_ps[:],
+                lhsT=h_codes[:, g * P : (g + 1) * P].bitcast(FP8X4),
+                lhsT_scale=h_scales[:, g * P : (g + 1) * P],
+                rhs=w1_codes[:, g, :].bitcast(FP8X4),
+                rhs_scale=w1_scales[:, g, :],
+                start=(g == 0),
+                stop=(g == PASSES1 - 1),
+            )
+        g_all = psum_once.tile([P, CF], F32)
+        spread(g_all, ROW_G)
+        b_all = psum_once.tile([P, CF], F32)
+        spread(b_all, ROW_B)
+        b2_ps = psum_turn.tile([P, CF], F32, tag="turn")
+        spread(b2_ps, ROW_B2)
+
+        w2_grouped = keep.tile([P, CF, PACK], BF16, align_bytes=64)
+        w2_codes = keep.tile([P, CF], U32, align_bytes=64)
+        w2_scales = keep.tile([P, CF], U8, align_bytes=64)
+        regroup(nc.scalar.copy, w2_grouped[:], w2_rows[:])
+
+        mu_pre = keep.tile([P, CODES, CF], F32)
+        row_sum = keep.tile([P, CODES], F32)
+        neg_mean = keep.tile([P, CODES], F32)
+        squares = keep.tile([P, CODES, CF], BF16)
+        sq_sum = keep.tile([P, CODES], F32)
+        for k in range(CODES):
+            one = slice(k, k + 1)
+            nc.vector.scalar_tensor_tensor(
+                out=mu_pre[:, k, :], in0=hp_ps[:], scalar=1.0, in1=c_all[:, k, :],
+                op0=ALU.mult, op1=ALU.add, accum_out=row_sum[:, one],
+            )
+            nc.scalar.mul(out=neg_mean[:, one], in_=row_sum[:, one], mul=-1.0 / CF)
+            nc.scalar.activation(
+                out=squares[:, k, :], in_=mu_pre[:, k, :], func=ACT.Square,
+                bias=neg_mean[:, one], scale=1.0, accum_out=sq_sum[:, one],
+            )
+        nc.vector.quantize_mx(
+            out=w2_codes[:].bitcast(FP8X4),
+            scales=w2_scales[:],
+            in_=w2_grouped[:].rearrange("p n j -> p (n j)"),
+        )
+        std = keep.tile([P, CODES], F32)
+        nc.scalar.activation(out=std[:], in_=sq_sum[:], func=ACT.Sqrt, bias=eps[:], scale=1.0 / CF)
+        nc.scalar.activation(out=table_warm[:, 1:2], in_=std[:, 0:1], func=ACT.Tanh)
+        b2_all = keep.tile([P, CF], F32)
+        nc.scalar.copy(out=b2_all[:], in_=b2_ps[:])
+
+        centred_g = keep.tile([P, CODES, CF], F32)
+        for k in range(CODES):
+            nc.vector.scalar_tensor_tensor(
+                out=centred_g[:, k, :], in0=mu_pre[:, k, :], scalar=neg_mean[:, k : k + 1],
+                in1=g_all[:], op0=ALU.add, op1=ALU.mult,
+            )
+        rstd = keep.tile([P, CODES], F32)
+        nc.vector.reciprocal(out=rstd[:], in_=std[:])
+
+        mu_ln = keep.tile([P, CODES, CF], BF16)
+        ln_grouped = keep.tile([P, CODES, P, PACK], BF16, align_bytes=64)
+        ln_codes = keep.tile([P, CODES, P], U32, align_bytes=64)
+        ln_scales = keep.tile([P, CODES, P], U8, align_bytes=64)
+        out_banks = {}
+        result = keep.tile([P, CODES, CF], F32)
+
+        def normalise_and_turn(k):
+            nc.vector.scalar_tensor_tensor(
+                out=mu_ln[:, k, :], in0=centred_g[:, k, :], scalar=rstd[:, k : k + 1],
+                in1=b_all[:], op0=ALU.mult, op1=ALU.add,
+            )
+            words = mu_ln[:, k, :].bitcast(F32)
+            lnT_ps = psum_turn.tile([P, 2, P], F32, tag="turn")
+            for u in range(2):
+                nc.tensor.transpose(lnT_ps[:, u, :], words[:, u : 2 * P : 2], ident_f32[:])
+            nc.scalar.copy(
+                out=ln_grouped[:, k].rearrange("p t j -> p (t j)").bitcast(F32).rearrange("p (t u) -> p t u", u=2),
+                in_=lnT_ps[:].rearrange("p u t -> p t u"),
+            )
+
+        def quantise_and_multiply(k):
+            nc.vector.quantize_mx(
+                out=ln_codes[:, k, :].bitcast(FP8X4),
+                scales=ln_scales[:, k, :],
+                in_=ln_grouped[:, k].rearrange("p t c -> p (t c)"),
+            )
+            out_ps = psum_out.tile([P, CF], F32)
+            out_banks[k] = out_ps
+            nc.tensor.matmul_mx(
+                out=out_ps[:],
+                lhsT=ln_codes[:, k, :].bitcast(FP8X4),
+                lhsT_scale=ln_scales[:, k, :],
+                rhs=w2_codes[:].bitcast(FP8X4),
+                rhs_scale=w2_scales[:],
+                start=True,
+                stop=True,
+            )
+
+        def finish(k):
+            nc.vector.tensor_tensor(
+                out=result[:, k, :], in0=out_banks[k][:], in1=b2_all[:], op=ALU.add
+            )
+            nc.scalar.activation(out=result[:, k, :], in_=result[:, k, :], func=ACT.Tanh)
+            nc.sync.dma_start(out=out_rows[:, k, :], in_=result[:, k, :])
+
+        for step in range(CODES + FINISH_LAG):
+            if step < CODES:
+                normalise_and_turn(step)
+            if 0 <= step - QUANTISE_LAG < CODES:
+                quantise_and_multiply(step - QUANTISE_LAG)
+            if step >= FINISH_LAG:
+                finish(step - FINISH_LAG)

@@ -17,13 +17,15 @@ D = 1024
 PASSES1 = D // (P * PACK)
 CODES = 4
 CF = 512
+CHUNKS = CF // P
 LN_EPS = 1e-5
 
-ROW_G, ROW_B, ROW_B2, ROW_B1 = 4, 5, 6, 7
-VECTORS = 8
+VEC_B1, VEC_G = 4, 5
+VECTORS = 6
+VEC_ROWS = VECTORS * CHUNKS
 
-QUANTISE_LAG = 2
-FINISH_LAG = 3
+W1_VECTOR = 288
+W2_SCALAR = 256
 
 FLOPS = 2 * P * D * CF + 2 * P * CODES * CF * CF
 
@@ -44,49 +46,48 @@ def tile_mixtureconfounderprior_pa_s_kernel(
 
     with ExitStack() as stack:
         keep = stack.enter_context(tc.tile_pool(name="keep", bufs=1))
-        psum_once = stack.enter_context(tc.psum_pool(name="psum_once", bufs=1))
-        psum_turn = stack.enter_context(tc.psum_pool(name="psum_turn", bufs=3))
-        psum_out = stack.enter_context(tc.psum_pool(name="psum_out", bufs=2))
+        psum = stack.enter_context(tc.psum_pool(name="psum", bufs=1))
         stack.enter_context(tc.manual_schedule())
 
-        vec_rows = keep.tile([P, CF], BF16)
-        nc.vector.memset(vec_rows[:], 0.0)
-        nc.sync.dma_start(out=vec_rows[0:CODES, :], in_=code_mu)
-        for row, vector in ((ROW_B1, mu_b1), (ROW_G, ln_g), (ROW_B, ln_b), (ROW_B2, mu_b2)):
-            nc.sync.dma_start(out=vec_rows[row : row + 1, :], in_=vector.unsqueeze(0))
+        vec_rows = keep.tile([P, P], BF16)
 
+        def load_vector(queue, v, rows):
+            first = v * CHUNKS
+            queue.dma_start(out=vec_rows[first : first + rows.shape[0], :], in_=rows)
+
+        nc.gpsimd.memset(vec_rows[:], 0.0)
         h_sb = keep.tile([P, D], BF16)
         nc.sync.dma_start(out=h_sb[:], in_=h_rows)
+        load_vector(nc.scalar, 0, code_mu.rearrange("k (c p) -> (k c) p", p=P))
+        load_vector(nc.sync, VEC_B1, mu_b1.rearrange("(c p) -> c p", p=P))
+        load_vector(nc.sync, VEC_G, ln_g.rearrange("(c p) -> c p", p=P))
         w1_rows = keep.tile([P, PASSES1, PACK, CF], BF16)
         w1_view = mu_w1_h.rearrange("(g p j) n -> g p j n", g=PASSES1, j=PACK)
         for g in range(PASSES1):
             nc.sync.dma_start(out=w1_rows[:, g], in_=w1_view[g])
         w2_rows = keep.tile([P, PACK, CF], BF16)
         nc.sync.dma_start(out=w2_rows[:], in_=mu_w2.rearrange("(p j) n -> p j n", j=PACK))
+        b_all = keep.tile([P, CF], BF16)
+        nc.sync.dma_start(out=b_all[:], in_=ln_b.partition_broadcast(P))
+        b2_all = keep.tile([P, CF], BF16)
+        nc.sync.dma_start(out=b2_all[:], in_=mu_b2.partition_broadcast(P))
 
-        ident_bf16 = keep.tile([P, P], BF16)
-        make_identity(nc, ident_bf16[:])
+        warm_in = keep.tile([P, 1], F32)
+        nc.vector.memset(warm_in[:], 1.0)
+        table_warm = keep.tile([P, 2], F32)
+        nc.scalar.activation(out=table_warm[:, 0:1], in_=warm_in[:], func=ACT.Sqrt)
+
         ident_f32 = keep.tile([P, P], F32)
         make_identity(nc, ident_f32[:])
-        eps = keep.tile([P, 1], F32)
-        nc.vector.memset(eps[:], LN_EPS)
-        table_warm = keep.tile([P, 2], F32)
-        nc.scalar.activation(out=table_warm[:, 0:1], in_=eps[:], func=ACT.Sqrt)
-
-        cols_ps = psum_turn.tile([P, PACK, P], BF16, tag="turn")
-        for c in range(PACK):
-            nc.tensor.transpose(cols_ps[:, c, :], vec_rows[:, c * P : (c + 1) * P], ident_bf16[:])
-        vec_cols = keep.tile([P, PACK, VECTORS], F32)
-        nc.vector.tensor_copy(out=vec_cols[:], in_=cols_ps[:, :, 0:VECTORS])
-        nc.vector.tensor_tensor(
-            out=vec_cols[:, :, 0:CODES],
-            in0=vec_cols[:, :, 0:CODES],
-            in1=vec_cols[:, :, ROW_B1 : ROW_B1 + 1].to_broadcast([P, PACK, CODES]),
-            op=ALU.add,
-        )
+        ident_bf16 = keep.tile([P, P], BF16)
+        make_identity(nc, ident_bf16[:])
+        neg_averager = keep.tile([P, P], BF16)
+        nc.gpsimd.memset(neg_averager[:], -1.0 / CF)
+        averager = keep.tile([P, P], F32)
+        nc.gpsimd.memset(averager[:], 1.0 / CF)
 
         h_words = h_sb[:].bitcast(F32)
-        hT_ps = psum_turn.tile([P, PASSES1, 2, P], F32, tag="turn")
+        hT_ps = psum.tile([P, PASSES1, 2, P], F32, tag="turn")
         for g in range(PASSES1):
             for u in range(2):
                 words = slice(2 * P * g + u, 2 * P * (g + 1), 2)
@@ -97,36 +98,74 @@ def tile_mixtureconfounderprior_pa_s_kernel(
             in_=hT_ps[:].rearrange("p g u t -> p g t u"),
         )
 
-        def spread(all_ps, j):
-            for c in range(PACK):
+        cols_ps = psum.tile([P, P], BF16, tag="small")
+        nc.tensor.transpose(cols_ps[:], vec_rows[:], ident_bf16[:])
+        vec_cols = keep.tile([P, VECTORS, CHUNKS], BF16)
+        nc.vector.tensor_copy(
+            out=vec_cols[:].rearrange("p v c -> p (v c)"), in_=cols_ps[:, 0:VEC_ROWS]
+        )
+
+        shape = [P, CODES, CHUNKS]
+        c_hat_ps = psum.tile(shape, F32, tag="small")
+        terms = [
+            (ident_bf16, vec_cols[:, 0:CODES, :]),
+            (ident_bf16, vec_cols[:, VEC_B1 : VEC_B1 + 1, :].to_broadcast(shape)),
+        ]
+        for c in range(CHUNKS):
+            terms.append((neg_averager, vec_cols[:, 0:CODES, c : c + 1].to_broadcast(shape)))
+            terms.append(
+                (neg_averager, vec_cols[:, VEC_B1 : VEC_B1 + 1, c : c + 1].to_broadcast(shape))
+            )
+        for i, (weights, columns) in enumerate(terms):
+            nc.tensor.matmul(
+                c_hat_ps[:], weights[:], columns, start=(i == 0), stop=(i == len(terms) - 1)
+            )
+
+        def spread(all_ps, columns, ident):
+            for c in range(CHUNKS):
                 nc.tensor.transpose(
                     all_ps[:, c * P : (c + 1) * P],
-                    vec_cols[:, c, j : j + 1].to_broadcast([P, P]),
-                    ident_f32[:],
+                    columns[:, c : c + 1].to_broadcast([P, P]),
+                    ident[:],
                 )
 
-        c_all = keep.tile([P, CODES, CF], F32)
-        for k in range(CODES):
-            c_ps = psum_turn.tile([P, CF], F32, tag="turn")
-            spread(c_ps, k)
-            nc.scalar.copy(out=c_all[:, k, :], in_=c_ps[:])
+        g_ps = psum.tile([P, CF], BF16, tag="vec")
+        spread(g_ps, vec_cols[:, VEC_G, :], ident_bf16)
 
         h_codes = keep.tile([P, PASSES1 * P], U32, align_bytes=64)
         h_scales = keep.tile([P, PASSES1 * P], U8, align_bytes=64)
         w1_grouped = keep.tile([P, PASSES1, CF, PACK], BF16, align_bytes=64)
         w1_codes = keep.tile([P, PASSES1, CF], U32, align_bytes=64)
         w1_scales = keep.tile([P, PASSES1, CF], U8, align_bytes=64)
-        regroup(nc.vector.tensor_copy, w1_grouped[:, 0], w1_rows[:, 0])
+        for g in range(PASSES1):
+            regroup(nc.scalar.copy, w1_grouped[:, g, W1_VECTOR:], w1_rows[:, g, :, W1_VECTOR:])
+        regroup(nc.vector.tensor_copy, w1_grouped[:, 0, :W1_VECTOR], w1_rows[:, 0, :, :W1_VECTOR])
+        c_hat_g = keep.tile(shape, F32)
+        nc.vector.tensor_tensor(
+            out=c_hat_g[:], in0=c_hat_ps[:],
+            in1=vec_cols[:, VEC_G : VEC_G + 1, :].to_broadcast(shape), op=ALU.mult,
+        )
+        cg_ps = []
+        for k in range(CODES):
+            one_ps = psum.tile([P, CF], F32, tag="code%d" % k, name="cg_ps%d" % k)
+            spread(one_ps, c_hat_g[:, k, :], ident_f32)
+            cg_ps.append(one_ps)
         nc.vector.quantize_mx(out=h_codes[:].bitcast(FP8X4), scales=h_scales[:], in_=h_grouped[:])
-        regroup(nc.vector.tensor_copy, w1_grouped[:, 1], w1_rows[:, 1])
+        regroup(nc.vector.tensor_copy, w1_grouped[:, 1, :W1_VECTOR], w1_rows[:, 1, :, :W1_VECTOR])
         for g in range(PASSES1):
             nc.vector.quantize_mx(
                 out=w1_codes[:, g, :].bitcast(FP8X4),
                 scales=w1_scales[:, g, :],
                 in_=w1_grouped[:, g].rearrange("p n j -> p (n j)"),
             )
+        c_hat_2 = keep.tile(shape, F32)
+        nc.scalar.mul(out=c_hat_2[:], in_=c_hat_ps[:], mul=2.0 / CF)
+        c_hat_sq = keep.tile(shape, F32)
+        nc.scalar.activation(out=c_hat_sq[:], in_=c_hat_ps[:], func=ACT.Square)
+        g_all = keep.tile([P, CF], BF16)
+        nc.scalar.copy(out=g_all[:], in_=g_ps[:])
 
-        hp_ps = psum_once.tile([P, CF], F32)
+        hp_ps = psum.tile([P, CF], F32, tag="hp")
         for g in range(PASSES1):
             nc.tensor.matmul_mx(
                 out=hp_ps[:],
@@ -137,60 +176,87 @@ def tile_mixtureconfounderprior_pa_s_kernel(
                 start=(g == 0),
                 stop=(g == PASSES1 - 1),
             )
-        g_all = psum_once.tile([P, CF], F32)
-        spread(g_all, ROW_G)
-        b_all = psum_once.tile([P, CF], F32)
-        spread(b_all, ROW_B)
-        b2_ps = psum_turn.tile([P, CF], F32, tag="turn")
-        spread(b2_ps, ROW_B2)
+        hpT_ps = psum.tile([P, CHUNKS, P], F32, tag="turn")
+        for c in range(CHUNKS):
+            for g in range(PASSES1):
+                nc.tensor.matmul_mx(
+                    out=hpT_ps[:, c, :],
+                    lhsT=w1_codes[:, g, c * P : (c + 1) * P].bitcast(FP8X4),
+                    lhsT_scale=w1_scales[:, g, c * P : (c + 1) * P],
+                    rhs=h_codes[:, g * P : (g + 1) * P].bitcast(FP8X4),
+                    rhs_scale=h_scales[:, g * P : (g + 1) * P],
+                    start=(g == 0),
+                    stop=(g == PASSES1 - 1),
+                )
 
         w2_grouped = keep.tile([P, CF, PACK], BF16, align_bytes=64)
         w2_codes = keep.tile([P, CF], U32, align_bytes=64)
         w2_scales = keep.tile([P, CF], U8, align_bytes=64)
-        regroup(nc.scalar.copy, w2_grouped[:], w2_rows[:])
-
-        mu_pre = keep.tile([P, CODES, CF], F32)
-        row_sum = keep.tile([P, CODES], F32)
-        neg_mean = keep.tile([P, CODES], F32)
-        squares = keep.tile([P, CODES, CF], BF16)
-        sq_sum = keep.tile([P, CODES], F32)
-        for k in range(CODES):
-            one = slice(k, k + 1)
-            nc.vector.scalar_tensor_tensor(
-                out=mu_pre[:, k, :], in0=hp_ps[:], scalar=1.0, in1=c_all[:, k, :],
-                op0=ALU.mult, op1=ALU.add, accum_out=row_sum[:, one],
-            )
-            nc.scalar.mul(out=neg_mean[:, one], in_=row_sum[:, one], mul=-1.0 / CF)
-            nc.scalar.activation(
-                out=squares[:, k, :], in_=mu_pre[:, k, :], func=ACT.Square,
-                bias=neg_mean[:, one], scale=1.0, accum_out=sq_sum[:, one],
-            )
+        regroup(nc.scalar.copy, w2_grouped[:, :W2_SCALAR], w2_rows[:, :, :W2_SCALAR])
+        regroup(nc.vector.tensor_copy, w2_grouped[:, W2_SCALAR:], w2_rows[:, :, W2_SCALAR:])
         nc.vector.quantize_mx(
             out=w2_codes[:].bitcast(FP8X4),
             scales=w2_scales[:],
             in_=w2_grouped[:].rearrange("p n j -> p (n j)"),
         )
-        std = keep.tile([P, CODES], F32)
-        nc.scalar.activation(out=std[:], in_=sq_sum[:], func=ACT.Sqrt, bias=eps[:], scale=1.0 / CF)
-        nc.scalar.activation(out=table_warm[:, 1:2], in_=std[:, 0:1], func=ACT.Tanh)
-        b2_all = keep.tile([P, CF], F32)
-        nc.scalar.copy(out=b2_all[:], in_=b2_ps[:])
+
+        unread = keep.tile([P, 2, CF], BF16)
+        hp_sum = keep.tile([P, 1], F32)
+        nc.scalar.activation(
+            out=unread[:, 0, :], in_=hp_ps[:], func=ACT.Identity, accum_out=hp_sum[:]
+        )
+        neg_mean = keep.tile([P, 1], F32)
+        nc.scalar.mul(out=neg_mean[:], in_=hp_sum[:], mul=-1.0 / CF)
+        hpT = keep.tile([P, CHUNKS, P], F32)
+        nc.scalar.copy(out=hpT[:], in_=hpT_ps[:])
+        hp_g = keep.tile([P, CF], F32)
+        nc.vector.scalar_tensor_tensor(
+            out=hp_g[:], in0=hp_ps[:], scalar=neg_mean[:], in1=g_all[:],
+            op0=ALU.add, op1=ALU.mult,
+        )
+        hp_sq = keep.tile([P, 1], F32)
+        nc.scalar.activation(
+            out=unread[:, 1, :], in_=hp_ps[:], func=ACT.Square, bias=neg_mean[:], scale=1.0,
+            accum_out=hp_sq[:],
+        )
+        hp_var_eps = keep.tile([P, 1], F32)
+        nc.scalar.activation(
+            out=hp_var_eps[:], in_=hp_sq[:], func=ACT.Identity, bias=LN_EPS, scale=1.0 / CF
+        )
+        var_ps = psum.tile([P, CODES], F32, tag="small")
+        for c in range(CHUNKS):
+            nc.tensor.matmul(
+                var_ps[:], averager[:], c_hat_sq[:, :, c], start=(c == 0), stop=False
+            )
+        for c in range(CHUNKS):
+            nc.tensor.matmul(
+                var_ps[:], hpT[:, c, :], c_hat_2[:, :, c], start=False, stop=(c == CHUNKS - 1)
+            )
 
         centred_g = keep.tile([P, CODES, CF], F32)
-        for k in range(CODES):
-            nc.vector.scalar_tensor_tensor(
-                out=centred_g[:, k, :], in0=mu_pre[:, k, :], scalar=neg_mean[:, k : k + 1],
-                in1=g_all[:], op0=ALU.add, op1=ALU.mult,
+
+        def add_code(k):
+            nc.vector.tensor_tensor(
+                out=centred_g[:, k, :], in0=hp_g[:], in1=cg_ps[k][:], op=ALU.add
             )
+
+        std = keep.tile([P, CODES], F32)
+        nc.scalar.activation(
+            out=std[:], in_=var_ps[:], func=ACT.Sqrt, bias=hp_var_eps[:], scale=1.0
+        )
+        nc.scalar.activation(out=table_warm[:, 1:2], in_=std[:, 0:1], func=ACT.Tanh)
         rstd = keep.tile([P, CODES], F32)
+        for k in range(CODES - 1):
+            add_code(k)
         nc.vector.reciprocal(out=rstd[:], in_=std[:])
 
         mu_ln = keep.tile([P, CODES, CF], BF16)
-        ln_grouped = keep.tile([P, CODES, P, PACK], BF16, align_bytes=64)
+        ln_grouped = keep.tile([P, CODES, P * PACK], BF16, align_bytes=64)
         ln_codes = keep.tile([P, CODES, P], U32, align_bytes=64)
         ln_scales = keep.tile([P, CODES, P], U8, align_bytes=64)
-        out_banks = {}
+        out_banks = []
         result = keep.tile([P, CODES, CF], F32)
+        free_banks = ("turn", "hp", "small", "vec")
 
         def normalise_and_turn(k):
             nc.vector.scalar_tensor_tensor(
@@ -198,11 +264,11 @@ def tile_mixtureconfounderprior_pa_s_kernel(
                 in1=b_all[:], op0=ALU.mult, op1=ALU.add,
             )
             words = mu_ln[:, k, :].bitcast(F32)
-            lnT_ps = psum_turn.tile([P, 2, P], F32, tag="turn")
+            lnT_ps = psum.tile([P, 2, P], F32, tag="code%d" % k, name="lnT_ps%d" % k)
             for u in range(2):
                 nc.tensor.transpose(lnT_ps[:, u, :], words[:, u : 2 * P : 2], ident_f32[:])
             nc.scalar.copy(
-                out=ln_grouped[:, k].rearrange("p t j -> p (t j)").bitcast(F32).rearrange("p (t u) -> p t u", u=2),
+                out=ln_grouped[:, k, :].bitcast(F32).rearrange("p (t u) -> p t u", u=2),
                 in_=lnT_ps[:].rearrange("p u t -> p t u"),
             )
 
@@ -210,10 +276,10 @@ def tile_mixtureconfounderprior_pa_s_kernel(
             nc.vector.quantize_mx(
                 out=ln_codes[:, k, :].bitcast(FP8X4),
                 scales=ln_scales[:, k, :],
-                in_=ln_grouped[:, k].rearrange("p t c -> p (t c)"),
+                in_=ln_grouped[:, k, :],
             )
-            out_ps = psum_out.tile([P, CF], F32)
-            out_banks[k] = out_ps
+            out_ps = psum.tile([P, CF], F32, tag=free_banks[k], name="out_ps%d" % k)
+            out_banks.append(out_ps)
             nc.tensor.matmul_mx(
                 out=out_ps[:],
                 lhsT=ln_codes[:, k, :].bitcast(FP8X4),
@@ -231,10 +297,12 @@ def tile_mixtureconfounderprior_pa_s_kernel(
             nc.scalar.activation(out=result[:, k, :], in_=result[:, k, :], func=ACT.Tanh)
             nc.sync.dma_start(out=out_rows[:, k, :], in_=result[:, k, :])
 
-        for step in range(CODES + FINISH_LAG):
+        for step in range(CODES + 2):
             if step < CODES:
                 normalise_and_turn(step)
-            if 0 <= step - QUANTISE_LAG < CODES:
-                quantise_and_multiply(step - QUANTISE_LAG)
-            if step >= FINISH_LAG:
-                finish(step - FINISH_LAG)
+            if step == 0:
+                add_code(CODES - 1)
+            if 0 <= step - 1 < CODES:
+                quantise_and_multiply(step - 1)
+            if step >= 2:
+                finish(step - 2)

@@ -24,8 +24,8 @@ VEC_B1, VEC_G = 4, 5
 VECTORS = 6
 VEC_ROWS = VECTORS * CHUNKS
 
-W1_VECTOR = 288
-W2_SCALAR = 256
+W1_VECTOR = (352, 288)
+W2_SCALAR = 288
 
 FLOPS = 2 * P * D * CF + 2 * P * CODES * CF * CF
 
@@ -75,7 +75,9 @@ def tile_mixtureconfounderprior_pa_s_kernel(
         warm_in = keep.tile([P, 1], F32)
         nc.vector.memset(warm_in[:], 1.0)
         table_warm = keep.tile([P, 2], F32)
-        nc.scalar.activation(out=table_warm[:, 0:1], in_=warm_in[:], func=ACT.Sqrt)
+        nc.scalar.activation(
+            out=table_warm[:, 0:1], in_=warm_in[:], func=ACT.Abs_reciprocal_sqrt
+        )
 
         ident_f32 = keep.tile([P, P], F32)
         make_identity(nc, ident_f32[:])
@@ -121,52 +123,88 @@ def tile_mixtureconfounderprior_pa_s_kernel(
                 c_hat_ps[:], weights[:], columns, start=(i == 0), stop=(i == len(terms) - 1)
             )
 
-        def spread(all_ps, columns, ident):
-            for c in range(CHUNKS):
-                nc.tensor.transpose(
-                    all_ps[:, c * P : (c + 1) * P],
-                    columns[:, c : c + 1].to_broadcast([P, P]),
-                    ident[:],
-                )
-
-        g_ps = psum.tile([P, CF], BF16, tag="vec")
-        spread(g_ps, vec_cols[:, VEC_G, :], ident_bf16)
+        g_cols = keep.tile([P, CHUNKS], F32)
+        nc.gpsimd.tensor_copy(out=g_cols[:], in_=vec_cols[:, VEC_G, :])
+        neg_g_cols = keep.tile([P, CHUNKS], F32)
+        nc.gpsimd.tensor_scalar(
+            out=neg_g_cols[:], in0=g_cols[:], scalar1=-1.0, scalar2=0.0, op0=ALU.mult, op1=ALU.add
+        )
 
         h_codes = keep.tile([P, PASSES1 * P], U32, align_bytes=64)
         h_scales = keep.tile([P, PASSES1 * P], U8, align_bytes=64)
         w1_grouped = keep.tile([P, PASSES1, CF, PACK], BF16, align_bytes=64)
         w1_codes = keep.tile([P, PASSES1, CF], U32, align_bytes=64)
         w1_scales = keep.tile([P, PASSES1, CF], U8, align_bytes=64)
-        for g in range(PASSES1):
-            regroup(nc.scalar.copy, w1_grouped[:, g, W1_VECTOR:], w1_rows[:, g, :, W1_VECTOR:])
-        regroup(nc.vector.tensor_copy, w1_grouped[:, 0, :W1_VECTOR], w1_rows[:, 0, :, :W1_VECTOR])
-        c_hat_g = keep.tile(shape, F32)
-        nc.vector.tensor_tensor(
-            out=c_hat_g[:], in0=c_hat_ps[:],
-            in1=vec_cols[:, VEC_G : VEC_G + 1, :].to_broadcast(shape), op=ALU.mult,
-        )
-        cg_ps = []
-        for k in range(CODES):
-            one_ps = psum.tile([P, CF], F32, tag="code%d" % k, name="cg_ps%d" % k)
-            spread(one_ps, c_hat_g[:, k, :], ident_f32)
-            cg_ps.append(one_ps)
-        nc.vector.quantize_mx(out=h_codes[:].bitcast(FP8X4), scales=h_scales[:], in_=h_grouped[:])
-        regroup(nc.vector.tensor_copy, w1_grouped[:, 1, :W1_VECTOR], w1_rows[:, 1, :, :W1_VECTOR])
-        for g in range(PASSES1):
+        def regroup_w1(g):
+            cut = W1_VECTOR[g]
+            regroup(nc.vector.tensor_copy, w1_grouped[:, g, :cut], w1_rows[:, g, :, :cut])
+            regroup(nc.scalar.copy, w1_grouped[:, g, cut:], w1_rows[:, g, :, cut:])
+
+        def quantise_w1(g):
             nc.vector.quantize_mx(
                 out=w1_codes[:, g, :].bitcast(FP8X4),
                 scales=w1_scales[:, g, :],
                 in_=w1_grouped[:, g].rearrange("p n j -> p (n j)"),
             )
+
+        regroup_w1(0)
+        c_hat_g = keep.tile(shape, F32)
+        nc.vector.tensor_tensor(
+            out=c_hat_g[:], in0=c_hat_ps[:],
+            in1=vec_cols[:, VEC_G : VEC_G + 1, :].to_broadcast(shape), op=ALU.mult,
+        )
         c_hat_2 = keep.tile(shape, F32)
         nc.scalar.mul(out=c_hat_2[:], in_=c_hat_ps[:], mul=2.0 / CF)
         c_hat_sq = keep.tile(shape, F32)
         nc.scalar.activation(out=c_hat_sq[:], in_=c_hat_ps[:], func=ACT.Square)
-        g_all = keep.tile([P, CF], BF16)
-        nc.scalar.copy(out=g_all[:], in_=g_ps[:])
+        c_sq_pairs = keep.tile([P, CODES, 2], F32)
+        nc.gpsimd.tensor_tensor(
+            out=c_sq_pairs[:], in0=c_hat_sq[:, :, 0:2], in1=c_hat_sq[:, :, 2:4], op=ALU.add
+        )
+        c_sq_sum = keep.tile([P, CODES], F32)
+        nc.gpsimd.tensor_tensor(
+            out=c_sq_sum[:], in0=c_sq_pairs[:, :, 0], in1=c_sq_pairs[:, :, 1], op=ALU.add
+        )
+        c_sq_eps = keep.tile([P, CODES], F32)
+        nc.gpsimd.tensor_scalar(
+            out=c_sq_eps[:], in0=c_sq_sum[:], scalar1=CHUNKS * LN_EPS, scalar2=1.0,
+            op0=ALU.add, op1=ALU.mult,
+        )
+        sum_ps = []
 
+        def open_sum(k):
+            one_ps = psum.tile([P, CF], F32, tag="code%d" % k, name="sum_ps%d" % k)
+            for c in range(CHUNKS):
+                nc.tensor.matmul(
+                    one_ps[:, c * P : (c + 1) * P],
+                    c_hat_g[:, k, c : c + 1].to_broadcast([P, P]),
+                    ident_f32[:],
+                    start=(c == 0),
+                    stop=False,
+                    is_transpose=True,
+                )
+            sum_ps.append(one_ps)
+
+        def close_sum(k):
+            for c in range(CHUNKS):
+                nc.tensor.matmul(
+                    sum_ps[k][:, c * P : (c + 1) * P],
+                    hpT_hat_g[:, c, :],
+                    ident_f32[:],
+                    start=False,
+                    stop=(c == CHUNKS - 1),
+                    is_transpose=True,
+                )
+
+        open_sum(0)
+        nc.vector.quantize_mx(out=h_codes[:].bitcast(FP8X4), scales=h_scales[:], in_=h_grouped[:])
+        regroup_w1(1)
+        quantise_w1(0)
+        quantise_w1(1)
         hp_ps = psum.tile([P, CF], F32, tag="hp")
         for g in range(PASSES1):
+            if g == PASSES1 - 1:
+                open_sum(1)
             nc.tensor.matmul_mx(
                 out=hp_ps[:],
                 lhsT=h_codes[:, g * P : (g + 1) * P].bitcast(FP8X4),
@@ -189,66 +227,58 @@ def tile_mixtureconfounderprior_pa_s_kernel(
                     stop=(g == PASSES1 - 1),
                 )
 
+        open_sum(2)
+        var_ps = psum.tile([P, CODES], F32, tag="vec")
+        nc.tensor.matmul(var_ps[:], averager[:], c_sq_eps[:], start=True, stop=False)
+
         w2_grouped = keep.tile([P, CF, PACK], BF16, align_bytes=64)
         w2_codes = keep.tile([P, CF], U32, align_bytes=64)
         w2_scales = keep.tile([P, CF], U8, align_bytes=64)
         regroup(nc.scalar.copy, w2_grouped[:, :W2_SCALAR], w2_rows[:, :, :W2_SCALAR])
+
+        hp_stats = keep.tile([P, 6], F32)
+        nc.vector.bn_stats(out=hp_stats[:], in_=hp_ps[:])
+        hp_mean_var = keep.tile([P, 2], F32)
+        nc.vector.bn_aggr(out=hp_mean_var[:], in_=hp_stats[:])
         regroup(nc.vector.tensor_copy, w2_grouped[:, W2_SCALAR:], w2_rows[:, :, W2_SCALAR:])
+
+        hpT = keep.tile([P, CHUNKS, P], F32)
+        nc.scalar.copy(out=hpT[:], in_=hpT_ps[:])
+        hpT_g = keep.tile([P, CHUNKS, P], F32)
+        for c in range(CHUNKS):
+            nc.scalar.mul(out=hpT_g[:, c, :], in_=hpT[:, c, :], mul=g_cols[:, c : c + 1])
+        mean_ps = psum.tile([P, P], F32, tag="small")
+        nc.tensor.transpose(
+            mean_ps[:], hp_mean_var[:, 0:1].to_broadcast([P, P]), ident_f32[:]
+        )
+        hpT_hat_g = keep.tile([P, CHUNKS, P], F32)
+        for c in range(CHUNKS):
+            nc.vector.scalar_tensor_tensor(
+                out=hpT_hat_g[:, c, :], in0=mean_ps[:], scalar=neg_g_cols[:, c : c + 1],
+                in1=hpT_g[:, c, :], op0=ALU.mult, op1=ALU.add,
+            )
+
+        for c in range(CHUNKS):
+            nc.tensor.matmul(
+                var_ps[:], hpT[:, c, :], c_hat_2[:, :, c], start=False, stop=(c == CHUNKS - 1)
+            )
+        rstd = keep.tile([P, CODES], F32)
+        nc.scalar.activation(
+            out=rstd[:], in_=var_ps[:], func=ACT.Abs_reciprocal_sqrt, bias=hp_mean_var[:, 1:2],
+            scale=1.0,
+        )
+        nc.scalar.activation(out=table_warm[:, 1:2], in_=rstd[:, 0:1], func=ACT.Tanh)
         nc.vector.quantize_mx(
             out=w2_codes[:].bitcast(FP8X4),
             scales=w2_scales[:],
             in_=w2_grouped[:].rearrange("p n j -> p (n j)"),
         )
 
-        unread = keep.tile([P, 2, CF], BF16)
-        hp_sum = keep.tile([P, 1], F32)
-        nc.scalar.activation(
-            out=unread[:, 0, :], in_=hp_ps[:], func=ACT.Identity, accum_out=hp_sum[:]
-        )
-        neg_mean = keep.tile([P, 1], F32)
-        nc.scalar.mul(out=neg_mean[:], in_=hp_sum[:], mul=-1.0 / CF)
-        hpT = keep.tile([P, CHUNKS, P], F32)
-        nc.scalar.copy(out=hpT[:], in_=hpT_ps[:])
-        hp_g = keep.tile([P, CF], F32)
-        nc.vector.scalar_tensor_tensor(
-            out=hp_g[:], in0=hp_ps[:], scalar=neg_mean[:], in1=g_all[:],
-            op0=ALU.add, op1=ALU.mult,
-        )
-        hp_sq = keep.tile([P, 1], F32)
-        nc.scalar.activation(
-            out=unread[:, 1, :], in_=hp_ps[:], func=ACT.Square, bias=neg_mean[:], scale=1.0,
-            accum_out=hp_sq[:],
-        )
-        hp_var_eps = keep.tile([P, 1], F32)
-        nc.scalar.activation(
-            out=hp_var_eps[:], in_=hp_sq[:], func=ACT.Identity, bias=LN_EPS, scale=1.0 / CF
-        )
-        var_ps = psum.tile([P, CODES], F32, tag="small")
-        for c in range(CHUNKS):
-            nc.tensor.matmul(
-                var_ps[:], averager[:], c_hat_sq[:, :, c], start=(c == 0), stop=False
-            )
-        for c in range(CHUNKS):
-            nc.tensor.matmul(
-                var_ps[:], hpT[:, c, :], c_hat_2[:, :, c], start=False, stop=(c == CHUNKS - 1)
-            )
-
-        centred_g = keep.tile([P, CODES, CF], F32)
-
-        def add_code(k):
-            nc.vector.tensor_tensor(
-                out=centred_g[:, k, :], in0=hp_g[:], in1=cg_ps[k][:], op=ALU.add
-            )
-
-        std = keep.tile([P, CODES], F32)
-        nc.scalar.activation(
-            out=std[:], in_=var_ps[:], func=ACT.Sqrt, bias=hp_var_eps[:], scale=1.0
-        )
-        nc.scalar.activation(out=table_warm[:, 1:2], in_=std[:, 0:1], func=ACT.Tanh)
-        rstd = keep.tile([P, CODES], F32)
-        for k in range(CODES - 1):
-            add_code(k)
-        nc.vector.reciprocal(out=rstd[:], in_=std[:])
+        close_sum(0)
+        close_sum(1)
+        close_sum(2)
+        open_sum(3)
+        close_sum(3)
 
         mu_ln = keep.tile([P, CODES, CF], BF16)
         ln_grouped = keep.tile([P, CODES, P * PACK], BF16, align_bytes=64)
@@ -260,7 +290,7 @@ def tile_mixtureconfounderprior_pa_s_kernel(
 
         def normalise_and_turn(k):
             nc.vector.scalar_tensor_tensor(
-                out=mu_ln[:, k, :], in0=centred_g[:, k, :], scalar=rstd[:, k : k + 1],
+                out=mu_ln[:, k, :], in0=sum_ps[k][:], scalar=rstd[:, k : k + 1],
                 in1=b_all[:], op0=ALU.mult, op1=ALU.add,
             )
             words = mu_ln[:, k, :].bitcast(F32)
@@ -290,19 +320,20 @@ def tile_mixtureconfounderprior_pa_s_kernel(
                 stop=True,
             )
 
-        def finish(k):
+        def add_bias(k):
             nc.vector.tensor_tensor(
                 out=result[:, k, :], in0=out_banks[k][:], in1=b2_all[:], op=ALU.add
             )
+
+        for k in range(CODES):
+            normalise_and_turn(k)
+        quantise_and_multiply(0)
+        quantise_and_multiply(1)
+        add_bias(0)
+        quantise_and_multiply(2)
+        quantise_and_multiply(3)
+        for k in range(CODES):
+            if k > 0:
+                add_bias(k)
             nc.scalar.activation(out=result[:, k, :], in_=result[:, k, :], func=ACT.Tanh)
             nc.sync.dma_start(out=out_rows[:, k, :], in_=result[:, k, :])
-
-        for step in range(CODES + 2):
-            if step < CODES:
-                normalise_and_turn(step)
-            if step == 0:
-                add_code(CODES - 1)
-            if 0 <= step - 1 < CODES:
-                quantise_and_multiply(step - 1)
-            if step >= 2:
-                finish(step - 2)

@@ -72,12 +72,20 @@ def tile_mixtureconfounderprior_pa_s_kernel(
         b2_all = keep.tile([P, CF], BF16)
         nc.sync.dma_start(out=b2_all[:], in_=mu_b2.partition_broadcast(P))
 
-        warm_in = keep.tile([P, 1], F32)
-        nc.vector.memset(warm_in[:], 1.0)
+        ones = keep.tile([P, P], F32)
+        nc.vector.memset(ones[:], 1.0)
         table_warm = keep.tile([P, 2], F32)
         nc.scalar.activation(
-            out=table_warm[:, 0:1], in_=warm_in[:], func=ACT.Abs_reciprocal_sqrt
+            out=table_warm[:, 0:1], in_=ones[:, 0:1], func=ACT.Abs_reciprocal_sqrt
         )
+
+        idle_ps = psum.tile([P, P], F32, tag="vec")
+
+        def keep_warm(times):
+            for i in range(times):
+                nc.tensor.matmul(idle_ps[:], ones[:], ones[:], start=True, stop=True)
+
+        keep_warm(3)
 
         ident_f32 = keep.tile([P, P], F32)
         make_identity(nc, ident_f32[:])
@@ -102,6 +110,7 @@ def tile_mixtureconfounderprior_pa_s_kernel(
 
         cols_ps = psum.tile([P, P], BF16, tag="small")
         nc.tensor.transpose(cols_ps[:], vec_rows[:], ident_bf16[:])
+        keep_warm(1)
         vec_cols = keep.tile([P, VECTORS, CHUNKS], BF16)
         nc.vector.tensor_copy(
             out=vec_cols[:].rearrange("p v c -> p (v c)"), in_=cols_ps[:, 0:VEC_ROWS]
@@ -123,6 +132,7 @@ def tile_mixtureconfounderprior_pa_s_kernel(
                 c_hat_ps[:], weights[:], columns, start=(i == 0), stop=(i == len(terms) - 1)
             )
 
+        keep_warm(1)
         g_cols = keep.tile([P, CHUNKS], F32)
         nc.gpsimd.tensor_copy(out=g_cols[:], in_=vec_cols[:, VEC_G, :])
         neg_g_cols = keep.tile([P, CHUNKS], F32)
@@ -197,6 +207,9 @@ def tile_mixtureconfounderprior_pa_s_kernel(
                 )
 
         open_sum(0)
+        keep_warm(1)
+        open_sum(1)
+        keep_warm(1)
         nc.vector.quantize_mx(out=h_codes[:].bitcast(FP8X4), scales=h_scales[:], in_=h_grouped[:])
         regroup_w1(1)
         quantise_w1(0)
@@ -204,7 +217,7 @@ def tile_mixtureconfounderprior_pa_s_kernel(
         hp_ps = psum.tile([P, CF], F32, tag="hp")
         for g in range(PASSES1):
             if g == PASSES1 - 1:
-                open_sum(1)
+                open_sum(2)
             nc.tensor.matmul_mx(
                 out=hp_ps[:],
                 lhsT=h_codes[:, g * P : (g + 1) * P].bitcast(FP8X4),
@@ -227,9 +240,9 @@ def tile_mixtureconfounderprior_pa_s_kernel(
                     stop=(g == PASSES1 - 1),
                 )
 
-        open_sum(2)
         var_ps = psum.tile([P, CODES], F32, tag="vec")
         nc.tensor.matmul(var_ps[:], averager[:], c_sq_eps[:], start=True, stop=False)
+        open_sum(3)
 
         w2_grouped = keep.tile([P, CF, PACK], BF16, align_bytes=64)
         w2_codes = keep.tile([P, CF], U32, align_bytes=64)
@@ -274,12 +287,6 @@ def tile_mixtureconfounderprior_pa_s_kernel(
             in_=w2_grouped[:].rearrange("p n j -> p (n j)"),
         )
 
-        close_sum(0)
-        close_sum(1)
-        close_sum(2)
-        open_sum(3)
-        close_sum(3)
-
         mu_ln = keep.tile([P, CODES, CF], BF16)
         ln_grouped = keep.tile([P, CODES, P * PACK], BF16, align_bytes=64)
         ln_codes = keep.tile([P, CODES, P], U32, align_bytes=64)
@@ -288,11 +295,13 @@ def tile_mixtureconfounderprior_pa_s_kernel(
         result = keep.tile([P, CODES, CF], F32)
         free_banks = ("turn", "hp", "small", "vec")
 
-        def normalise_and_turn(k):
+        def normalise(k):
             nc.vector.scalar_tensor_tensor(
                 out=mu_ln[:, k, :], in0=sum_ps[k][:], scalar=rstd[:, k : k + 1],
                 in1=b_all[:], op0=ALU.mult, op1=ALU.add,
             )
+
+        def turn(k):
             words = mu_ln[:, k, :].bitcast(F32)
             lnT_ps = psum.tile([P, 2, P], F32, tag="code%d" % k, name="lnT_ps%d" % k)
             for u in range(2):
@@ -325,12 +334,21 @@ def tile_mixtureconfounderprior_pa_s_kernel(
                 out=result[:, k, :], in0=out_banks[k][:], in1=b2_all[:], op=ALU.add
             )
 
-        for k in range(CODES):
-            normalise_and_turn(k)
+        for k in range(CODES - 1):
+            close_sum(k)
+        normalise(0)
+        turn(0)
+        close_sum(CODES - 1)
+        normalise(1)
+        turn(1)
+        normalise(2)
+        turn(2)
+        normalise(3)
         quantise_and_multiply(0)
+        turn(3)
         quantise_and_multiply(1)
-        add_bias(0)
         quantise_and_multiply(2)
+        add_bias(0)
         quantise_and_multiply(3)
         for k in range(CODES):
             if k > 0:

@@ -24,7 +24,7 @@ VEC_B1, VEC_G = 4, 5
 VECTORS = 6
 VEC_ROWS = VECTORS * CHUNKS
 
-W1_VECTOR = (352, 288)
+W1_VECTOR = (352, 272)
 W2_SCALAR = 288
 
 FLOPS = 2 * P * D * CF + 2 * P * CODES * CF * CF
@@ -137,7 +137,8 @@ def tile_mixtureconfounderprior_pa_s_kernel(
         nc.gpsimd.tensor_copy(out=g_cols[:], in_=vec_cols[:, VEC_G, :])
         neg_g_cols = keep.tile([P, CHUNKS], F32)
         nc.gpsimd.tensor_scalar(
-            out=neg_g_cols[:], in0=g_cols[:], scalar1=-1.0, scalar2=0.0, op0=ALU.mult, op1=ALU.add
+            out=neg_g_cols[:], in0=g_cols[:], scalar1=-1.0 / CF, scalar2=0.0,
+            op0=ALU.mult, op1=ALU.add,
         )
 
         h_codes = keep.tile([P, PASSES1 * P], U32, align_bytes=64)
@@ -210,14 +211,13 @@ def tile_mixtureconfounderprior_pa_s_kernel(
         keep_warm(1)
         open_sum(1)
         keep_warm(1)
+        open_sum(2)
         nc.vector.quantize_mx(out=h_codes[:].bitcast(FP8X4), scales=h_scales[:], in_=h_grouped[:])
         regroup_w1(1)
         quantise_w1(0)
         quantise_w1(1)
         hp_ps = psum.tile([P, CF], F32, tag="hp")
         for g in range(PASSES1):
-            if g == PASSES1 - 1:
-                open_sum(2)
             nc.tensor.matmul_mx(
                 out=hp_ps[:],
                 lhsT=h_codes[:, g * P : (g + 1) * P].bitcast(FP8X4),
@@ -249,25 +249,35 @@ def tile_mixtureconfounderprior_pa_s_kernel(
         w2_scales = keep.tile([P, CF], U8, align_bytes=64)
         regroup(nc.scalar.copy, w2_grouped[:, :W2_SCALAR], w2_rows[:, :, :W2_SCALAR])
 
+        unread = keep.tile([P, CF], BF16)
+        hp_sum = keep.tile([P, 1], F32)
+        nc.scalar.activation(
+            out=unread[:], in_=hp_ps[:], func=ACT.Identity, accum_out=hp_sum[:]
+        )
+        regroup(nc.vector.tensor_copy, w2_grouped[:, W2_SCALAR:], w2_rows[:, :, W2_SCALAR:])
         hp_stats = keep.tile([P, 6], F32)
         nc.vector.bn_stats(out=hp_stats[:], in_=hp_ps[:])
-        hp_mean_var = keep.tile([P, 2], F32)
-        nc.vector.bn_aggr(out=hp_mean_var[:], in_=hp_stats[:])
-        regroup(nc.vector.tensor_copy, w2_grouped[:, W2_SCALAR:], w2_rows[:, :, W2_SCALAR:])
 
         hpT = keep.tile([P, CHUNKS, P], F32)
-        nc.scalar.copy(out=hpT[:], in_=hpT_ps[:])
+        for first in (0, CHUNKS // 2):
+            half = slice(first, first + CHUNKS // 2)
+            nc.scalar.copy(out=hpT[:, half, :], in_=hpT_ps[:, half, :])
         hpT_g = keep.tile([P, CHUNKS, P], F32)
-        for c in range(CHUNKS):
+        for c in range(CHUNKS // 2):
             nc.scalar.mul(out=hpT_g[:, c, :], in_=hpT[:, c, :], mul=g_cols[:, c : c + 1])
-        mean_ps = psum.tile([P, P], F32, tag="small")
-        nc.tensor.transpose(
-            mean_ps[:], hp_mean_var[:, 0:1].to_broadcast([P, P]), ident_f32[:]
-        )
+        hp_mean_var = keep.tile([P, 2], F32)
+        nc.vector.bn_aggr(out=hp_mean_var[:], in_=hp_stats[:])
+        for c in range(CHUNKS // 2, CHUNKS):
+            nc.vector.tensor_scalar(
+                out=hpT_g[:, c, :], in0=hpT[:, c, :], scalar1=g_cols[:, c : c + 1], scalar2=None,
+                op0=ALU.mult,
+            )
+        sum_all_ps = psum.tile([P, P], F32, tag="small")
+        nc.tensor.transpose(sum_all_ps[:], hp_sum[:].to_broadcast([P, P]), ident_f32[:])
         hpT_hat_g = keep.tile([P, CHUNKS, P], F32)
         for c in range(CHUNKS):
             nc.vector.scalar_tensor_tensor(
-                out=hpT_hat_g[:, c, :], in0=mean_ps[:], scalar=neg_g_cols[:, c : c + 1],
+                out=hpT_hat_g[:, c, :], in0=sum_all_ps[:], scalar=neg_g_cols[:, c : c + 1],
                 in1=hpT_g[:, c, :], op0=ALU.mult, op1=ALU.add,
             )
 
@@ -329,10 +339,14 @@ def tile_mixtureconfounderprior_pa_s_kernel(
                 stop=True,
             )
 
-        def add_bias(k):
+        def add_bias(k, cols):
             nc.vector.tensor_tensor(
-                out=result[:, k, :], in0=out_banks[k][:], in1=b2_all[:], op=ALU.add
+                out=result[:, k, cols], in0=out_banks[k][:, cols], in1=b2_all[:, cols], op=ALU.add
             )
+
+        def finish(k, cols):
+            nc.scalar.activation(out=result[:, k, cols], in_=result[:, k, cols], func=ACT.Tanh)
+            nc.sync.dma_start(out=out_rows[:, k, cols], in_=result[:, k, cols])
 
         for k in range(CODES - 1):
             close_sum(k)
@@ -348,10 +362,13 @@ def tile_mixtureconfounderprior_pa_s_kernel(
         turn(3)
         quantise_and_multiply(1)
         quantise_and_multiply(2)
-        add_bias(0)
+        whole = slice(0, CF)
+        add_bias(0, whole)
         quantise_and_multiply(3)
-        for k in range(CODES):
-            if k > 0:
-                add_bias(k)
-            nc.scalar.activation(out=result[:, k, :], in_=result[:, k, :], func=ACT.Tanh)
-            nc.sync.dma_start(out=out_rows[:, k, :], in_=result[:, k, :])
+        finish(0, whole)
+        for k in range(1, CODES - 1):
+            add_bias(k, whole)
+            finish(k, whole)
+        for first in (0, CF // 2):
+            add_bias(CODES - 1, slice(first, first + CF // 2))
+            finish(CODES - 1, slice(first, first + CF // 2))

@@ -24,8 +24,8 @@ VEC_B1, VEC_G = 4, 5
 VECTORS = 6
 VEC_ROWS = VECTORS * CHUNKS
 
-W1_VECTOR = (352, 272)
-W2_SCALAR = 288
+W1_VECTOR = (352, 352)
+W2_VECTOR = 224
 
 FLOPS = 2 * P * D * CF + 2 * P * CODES * CF * CF
 
@@ -50,102 +50,89 @@ def tile_mixtureconfounderprior_pa_s_kernel(
         stack.enter_context(tc.manual_schedule())
 
         vec_rows = keep.tile([P, P], BF16)
-
-        def load_vector(queue, v, rows):
-            first = v * CHUNKS
-            queue.dma_start(out=vec_rows[first : first + rows.shape[0], :], in_=rows)
-
-        nc.gpsimd.memset(vec_rows[:], 0.0)
-        h_sb = keep.tile([P, D], BF16)
-        nc.sync.dma_start(out=h_sb[:], in_=h_rows)
-        load_vector(nc.scalar, 0, code_mu.rearrange("k (c p) -> (k c) p", p=P))
-        load_vector(nc.sync, VEC_B1, mu_b1.rearrange("(c p) -> c p", p=P))
-        load_vector(nc.sync, VEC_G, ln_g.rearrange("(c p) -> c p", p=P))
         w1_rows = keep.tile([P, PASSES1, PACK, CF], BF16)
-        w1_view = mu_w1_h.rearrange("(g p j) n -> g p j n", g=PASSES1, j=PACK)
-        for g in range(PASSES1):
-            nc.sync.dma_start(out=w1_rows[:, g], in_=w1_view[g])
+        h_sb = keep.tile([P, D], BF16)
         w2_rows = keep.tile([P, PACK, CF], BF16)
-        nc.sync.dma_start(out=w2_rows[:], in_=mu_w2.rearrange("(p j) n -> p j n", j=PACK))
         b_all = keep.tile([P, CF], BF16)
-        nc.sync.dma_start(out=b_all[:], in_=ln_b.partition_broadcast(P))
         b2_all = keep.tile([P, CF], BF16)
-        nc.sync.dma_start(out=b2_all[:], in_=mu_b2.partition_broadcast(P))
-
         ones = keep.tile([P, P], F32)
-        nc.vector.memset(ones[:], 1.0)
         table_warm = keep.tile([P, 2], F32)
-        nc.scalar.activation(
-            out=table_warm[:, 0:1], in_=ones[:, 0:1], func=ACT.Abs_reciprocal_sqrt
-        )
-
-        idle_ps = psum.tile([P, P], F32, tag="vec")
-
-        def keep_warm(times):
-            for i in range(times):
-                nc.tensor.matmul(idle_ps[:], ones[:], ones[:], start=True, stop=True)
-
-        keep_warm(3)
-
-        ident_f32 = keep.tile([P, P], F32)
-        make_identity(nc, ident_f32[:])
         ident_bf16 = keep.tile([P, P], BF16)
-        make_identity(nc, ident_bf16[:])
+        ident_f32 = keep.tile([P, P], F32)
         neg_averager = keep.tile([P, P], BF16)
-        nc.gpsimd.memset(neg_averager[:], -1.0 / CF)
         averager = keep.tile([P, P], F32)
-        nc.gpsimd.memset(averager[:], 1.0 / CF)
-
-        h_words = h_sb[:].bitcast(F32)
-        hT_ps = psum.tile([P, PASSES1, 2, P], F32, tag="turn")
-        for g in range(PASSES1):
-            for u in range(2):
-                words = slice(2 * P * g + u, 2 * P * (g + 1), 2)
-                nc.tensor.transpose(hT_ps[:, g, u, :], h_words[:, words], ident_f32[:])
-        h_grouped = keep.tile([P, PASSES1 * P * PACK], BF16, align_bytes=64)
-        nc.scalar.copy(
-            out=h_grouped[:].bitcast(F32).rearrange("p (g t u) -> p g t u", g=PASSES1, u=2),
-            in_=hT_ps[:].rearrange("p g u t -> p g t u"),
-        )
-
-        cols_ps = psum.tile([P, P], BF16, tag="small")
-        nc.tensor.transpose(cols_ps[:], vec_rows[:], ident_bf16[:])
-        keep_warm(1)
         vec_cols = keep.tile([P, VECTORS, CHUNKS], BF16)
-        nc.vector.tensor_copy(
-            out=vec_cols[:].rearrange("p v c -> p (v c)"), in_=cols_ps[:, 0:VEC_ROWS]
-        )
-
-        shape = [P, CODES, CHUNKS]
-        c_hat_ps = psum.tile(shape, F32, tag="small")
-        terms = [
-            (ident_bf16, vec_cols[:, 0:CODES, :]),
-            (ident_bf16, vec_cols[:, VEC_B1 : VEC_B1 + 1, :].to_broadcast(shape)),
-        ]
-        for c in range(CHUNKS):
-            terms.append((neg_averager, vec_cols[:, 0:CODES, c : c + 1].to_broadcast(shape)))
-            terms.append(
-                (neg_averager, vec_cols[:, VEC_B1 : VEC_B1 + 1, c : c + 1].to_broadcast(shape))
-            )
-        for i, (weights, columns) in enumerate(terms):
-            nc.tensor.matmul(
-                c_hat_ps[:], weights[:], columns, start=(i == 0), stop=(i == len(terms) - 1)
-            )
-
-        keep_warm(1)
         g_cols = keep.tile([P, CHUNKS], F32)
-        nc.gpsimd.tensor_copy(out=g_cols[:], in_=vec_cols[:, VEC_G, :])
         neg_g_cols = keep.tile([P, CHUNKS], F32)
-        nc.gpsimd.tensor_scalar(
-            out=neg_g_cols[:], in0=g_cols[:], scalar1=-1.0 / CF, scalar2=0.0,
-            op0=ALU.mult, op1=ALU.add,
-        )
-
+        by_code = [P, CODES, CHUNKS]
+        c_hat_g = keep.tile(by_code, F32)
+        c_hat_2 = keep.tile(by_code, F32)
+        c_hat_sq = keep.tile(by_code, F32)
+        c_sq_pairs = keep.tile([P, CODES, 2], F32)
+        c_sq_sum = keep.tile([P, CODES], F32)
+        c_sq_eps = keep.tile([P, CODES], F32)
+        h_grouped = keep.tile([P, PASSES1 * P * PACK], BF16, align_bytes=64)
         h_codes = keep.tile([P, PASSES1 * P], U32, align_bytes=64)
         h_scales = keep.tile([P, PASSES1 * P], U8, align_bytes=64)
         w1_grouped = keep.tile([P, PASSES1, CF, PACK], BF16, align_bytes=64)
         w1_codes = keep.tile([P, PASSES1, CF], U32, align_bytes=64)
         w1_scales = keep.tile([P, PASSES1, CF], U8, align_bytes=64)
+        w2_grouped = keep.tile([P, CF, PACK], BF16, align_bytes=64)
+        w2_codes = keep.tile([P, CF], U32, align_bytes=64)
+        w2_scales = keep.tile([P, CF], U8, align_bytes=64)
+        unread = keep.tile([P, CF], BF16)
+        hp_sum = keep.tile([P, 1], F32)
+        hp_stats = keep.tile([P, 6], F32)
+        hp_mean_var = keep.tile([P, 2], F32)
+        hpT = keep.tile([P, CHUNKS, P], F32)
+        hpT_g = keep.tile([P, CHUNKS, P], F32)
+        hpT_hat_g = keep.tile([P, CHUNKS, P], F32)
+        rstd = keep.tile([P, CODES], F32)
+        mu_ln = keep.tile([P, CODES, CF], BF16)
+        ln_grouped = keep.tile([P, CODES, P * PACK], BF16, align_bytes=64)
+        ln_codes = keep.tile([P, CODES, P], U32, align_bytes=64)
+        ln_scales = keep.tile([P, CODES, P], U8, align_bytes=64)
+        result = keep.tile([P, CODES, CF], F32)
+
+
+        bank = {}
+
+        def open_bank(name, tag, shape, dtype=F32):
+            bank[name] = psum.tile(shape, dtype, tag=tag, name=name)
+            return bank[name]
+
+        def load_vector(queue, v, rows):
+            first = v * CHUNKS
+            queue.dma_start(out=vec_rows[first : first + rows.shape[0], :], in_=rows)
+
+        def load_w1(g):
+            view = mu_w1_h.rearrange("(g p j) n -> g p j n", g=PASSES1, j=PACK)
+            nc.sync.dma_start(out=w1_rows[:, g], in_=view[g])
+
+        def load_w2():
+            nc.sync.dma_start(out=w2_rows[:], in_=mu_w2.rearrange("(p j) n -> p j n", j=PACK))
+
+        def keep_warm(times):
+            for i in range(times):
+                nc.tensor.matmul(bank["idle"][:], ones[:], ones[:], start=True, stop=True)
+
+        def turn_h():
+            h_words = h_sb[:].bitcast(F32)
+            hT_ps = open_bank("hT", "b0", [P, PASSES1, 2, P])
+            for g in range(PASSES1):
+                for u in range(2):
+                    words = slice(2 * P * g + u, 2 * P * (g + 1), 2)
+                    nc.tensor.transpose(hT_ps[:, g, u, :], h_words[:, words], ident_f32[:])
+            nc.scalar.copy(
+                out=h_grouped[:].bitcast(F32).rearrange("p (g t u) -> p g t u", g=PASSES1, u=2),
+                in_=hT_ps[:].rearrange("p g u t -> p g t u"),
+            )
+
+        def quantise_h():
+            nc.vector.quantize_mx(
+                out=h_codes[:].bitcast(FP8X4), scales=h_scales[:], in_=h_grouped[:]
+            )
+
         def regroup_w1(g):
             cut = W1_VECTOR[g]
             regroup(nc.vector.tensor_copy, w1_grouped[:, g, :cut], w1_rows[:, g, :, :cut])
@@ -158,48 +145,69 @@ def tile_mixtureconfounderprior_pa_s_kernel(
                 in_=w1_grouped[:, g].rearrange("p n j -> p (n j)"),
             )
 
-        regroup_w1(0)
-        c_hat_g = keep.tile(shape, F32)
-        nc.vector.tensor_tensor(
-            out=c_hat_g[:], in0=c_hat_ps[:],
-            in1=vec_cols[:, VEC_G : VEC_G + 1, :].to_broadcast(shape), op=ALU.mult,
-        )
-        c_hat_2 = keep.tile(shape, F32)
-        nc.scalar.mul(out=c_hat_2[:], in_=c_hat_ps[:], mul=2.0 / CF)
-        c_hat_sq = keep.tile(shape, F32)
-        nc.scalar.activation(out=c_hat_sq[:], in_=c_hat_ps[:], func=ACT.Square)
-        c_sq_pairs = keep.tile([P, CODES, 2], F32)
-        nc.gpsimd.tensor_tensor(
-            out=c_sq_pairs[:], in0=c_hat_sq[:, :, 0:2], in1=c_hat_sq[:, :, 2:4], op=ALU.add
-        )
-        c_sq_sum = keep.tile([P, CODES], F32)
-        nc.gpsimd.tensor_tensor(
-            out=c_sq_sum[:], in0=c_sq_pairs[:, :, 0], in1=c_sq_pairs[:, :, 1], op=ALU.add
-        )
-        c_sq_eps = keep.tile([P, CODES], F32)
-        nc.gpsimd.tensor_scalar(
-            out=c_sq_eps[:], in0=c_sq_sum[:], scalar1=CHUNKS * LN_EPS, scalar2=1.0,
-            op0=ALU.add, op1=ALU.mult,
-        )
-        sum_ps = []
+        def turn_vectors():
+            cols_ps = open_bank("cols", "b2", [P, P], BF16)
+            nc.tensor.transpose(cols_ps[:], vec_rows[:], ident_bf16[:])
+
+        def take_vectors():
+            nc.vector.tensor_copy(
+                out=vec_cols[:].rearrange("p v c -> p (v c)"), in_=bank["cols"][:, 0:VEC_ROWS]
+            )
+            nc.gpsimd.tensor_copy(out=g_cols[:], in_=vec_cols[:, VEC_G, :])
+            nc.gpsimd.tensor_scalar(
+                out=neg_g_cols[:], in0=g_cols[:], scalar1=-1.0 / CF, scalar2=0.0,
+                op0=ALU.mult, op1=ALU.add,
+            )
+
+        def centre_codes():
+            c_hat_ps = open_bank("c_hat", "b2", by_code)
+            codes = vec_cols[:, 0:CODES, :]
+            b1 = vec_cols[:, VEC_B1 : VEC_B1 + 1, :]
+            terms = [(ident_bf16, codes), (ident_bf16, b1.to_broadcast(by_code))]
+            for c in range(CHUNKS):
+                terms.append((neg_averager, codes[:, :, c : c + 1].to_broadcast(by_code)))
+                terms.append((neg_averager, b1[:, :, c : c + 1].to_broadcast(by_code)))
+            for i, (weights, columns) in enumerate(terms):
+                nc.tensor.matmul(
+                    c_hat_ps[:], weights[:], columns, start=(i == 0), stop=(i == len(terms) - 1)
+                )
+
+        def scale_codes():
+            nc.vector.tensor_tensor(
+                out=c_hat_g[:], in0=bank["c_hat"][:],
+                in1=vec_cols[:, VEC_G : VEC_G + 1, :].to_broadcast(by_code), op=ALU.mult,
+            )
+
+        def prepare_variances():
+            nc.scalar.mul(out=c_hat_2[:], in_=bank["c_hat"][:], mul=2.0 / CF)
+            nc.scalar.activation(out=c_hat_sq[:], in_=bank["c_hat"][:], func=ACT.Square)
+            nc.gpsimd.tensor_tensor(
+                out=c_sq_pairs[:], in0=c_hat_sq[:, :, 0:2], in1=c_hat_sq[:, :, 2:4], op=ALU.add
+            )
+            nc.gpsimd.tensor_tensor(
+                out=c_sq_sum[:], in0=c_sq_pairs[:, :, 0], in1=c_sq_pairs[:, :, 1], op=ALU.add
+            )
+            nc.gpsimd.tensor_scalar(
+                out=c_sq_eps[:], in0=c_sq_sum[:], scalar1=CHUNKS * LN_EPS, scalar2=1.0,
+                op0=ALU.add, op1=ALU.mult,
+            )
 
         def open_sum(k):
-            one_ps = psum.tile([P, CF], F32, tag="code%d" % k, name="sum_ps%d" % k)
+            sum_ps = open_bank("sum%d" % k, "b%d" % (4 + k), [P, CF])
             for c in range(CHUNKS):
                 nc.tensor.matmul(
-                    one_ps[:, c * P : (c + 1) * P],
+                    sum_ps[:, c * P : (c + 1) * P],
                     c_hat_g[:, k, c : c + 1].to_broadcast([P, P]),
                     ident_f32[:],
                     start=(c == 0),
                     stop=False,
                     is_transpose=True,
                 )
-            sum_ps.append(one_ps)
 
         def close_sum(k):
             for c in range(CHUNKS):
                 nc.tensor.matmul(
-                    sum_ps[k][:, c * P : (c + 1) * P],
+                    bank["sum%d" % k][:, c * P : (c + 1) * P],
                     hpT_hat_g[:, c, :],
                     ident_f32[:],
                     start=False,
@@ -207,19 +215,11 @@ def tile_mixtureconfounderprior_pa_s_kernel(
                     is_transpose=True,
                 )
 
-        open_sum(0)
-        keep_warm(1)
-        open_sum(1)
-        keep_warm(1)
-        open_sum(2)
-        nc.vector.quantize_mx(out=h_codes[:].bitcast(FP8X4), scales=h_scales[:], in_=h_grouped[:])
-        regroup_w1(1)
-        quantise_w1(0)
-        quantise_w1(1)
-        hp_ps = psum.tile([P, CF], F32, tag="hp")
-        for g in range(PASSES1):
+        def multiply_tokens(g):
+            if g == 0:
+                open_bank("hp", "b1", [P, CF])
             nc.tensor.matmul_mx(
-                out=hp_ps[:],
+                out=bank["hp"][:],
                 lhsT=h_codes[:, g * P : (g + 1) * P].bitcast(FP8X4),
                 lhsT_scale=h_scales[:, g * P : (g + 1) * P],
                 rhs=w1_codes[:, g, :].bitcast(FP8X4),
@@ -227,93 +227,94 @@ def tile_mixtureconfounderprior_pa_s_kernel(
                 start=(g == 0),
                 stop=(g == PASSES1 - 1),
             )
-        hpT_ps = psum.tile([P, CHUNKS, P], F32, tag="turn")
-        for c in range(CHUNKS):
-            for g in range(PASSES1):
-                nc.tensor.matmul_mx(
-                    out=hpT_ps[:, c, :],
-                    lhsT=w1_codes[:, g, c * P : (c + 1) * P].bitcast(FP8X4),
-                    lhsT_scale=w1_scales[:, g, c * P : (c + 1) * P],
-                    rhs=h_codes[:, g * P : (g + 1) * P].bitcast(FP8X4),
-                    rhs_scale=h_scales[:, g * P : (g + 1) * P],
-                    start=(g == 0),
-                    stop=(g == PASSES1 - 1),
-                )
 
-        var_ps = psum.tile([P, CODES], F32, tag="vec")
-        nc.tensor.matmul(var_ps[:], averager[:], c_sq_eps[:], start=True, stop=False)
-        open_sum(3)
+        def multiply_features():
+            hpT_ps = open_bank("hpT", "b0", [P, CHUNKS, P])
+            for c in range(CHUNKS):
+                for g in range(PASSES1):
+                    nc.tensor.matmul_mx(
+                        out=hpT_ps[:, c, :],
+                        lhsT=w1_codes[:, g, c * P : (c + 1) * P].bitcast(FP8X4),
+                        lhsT_scale=w1_scales[:, g, c * P : (c + 1) * P],
+                        rhs=h_codes[:, g * P : (g + 1) * P].bitcast(FP8X4),
+                        rhs_scale=h_scales[:, g * P : (g + 1) * P],
+                        start=(g == 0),
+                        stop=(g == PASSES1 - 1),
+                    )
 
-        w2_grouped = keep.tile([P, CF, PACK], BF16, align_bytes=64)
-        w2_codes = keep.tile([P, CF], U32, align_bytes=64)
-        w2_scales = keep.tile([P, CF], U8, align_bytes=64)
-        regroup(nc.scalar.copy, w2_grouped[:, :W2_SCALAR], w2_rows[:, :, :W2_SCALAR])
+        def regroup_w2_scalar():
+            regroup(nc.scalar.copy, w2_grouped[:, W2_VECTOR:], w2_rows[:, :, W2_VECTOR:])
 
-        unread = keep.tile([P, CF], BF16)
-        hp_sum = keep.tile([P, 1], F32)
-        nc.scalar.activation(
-            out=unread[:], in_=hp_ps[:], func=ACT.Identity, accum_out=hp_sum[:]
-        )
-        regroup(nc.vector.tensor_copy, w2_grouped[:, W2_SCALAR:], w2_rows[:, :, W2_SCALAR:])
-        hp_stats = keep.tile([P, 6], F32)
-        nc.vector.bn_stats(out=hp_stats[:], in_=hp_ps[:])
+        def regroup_w2_vector():
+            regroup(nc.vector.tensor_copy, w2_grouped[:, :W2_VECTOR], w2_rows[:, :, :W2_VECTOR])
 
-        hpT = keep.tile([P, CHUNKS, P], F32)
-        for first in (0, CHUNKS // 2):
-            half = slice(first, first + CHUNKS // 2)
-            nc.scalar.copy(out=hpT[:, half, :], in_=hpT_ps[:, half, :])
-        hpT_g = keep.tile([P, CHUNKS, P], F32)
-        for c in range(CHUNKS // 2):
+        def quantise_w2():
+            nc.vector.quantize_mx(
+                out=w2_codes[:].bitcast(FP8X4),
+                scales=w2_scales[:],
+                in_=w2_grouped[:].rearrange("p n j -> p (n j)"),
+            )
+
+        def sum_hp():
+            nc.scalar.activation(
+                out=unread[:], in_=bank["hp"][:], func=ACT.Identity, accum_out=hp_sum[:]
+            )
+
+        def spread_hp_sum():
+            sum_all_ps = open_bank("sum_all", "b2", [P, P])
+            nc.tensor.transpose(sum_all_ps[:], hp_sum[:].to_broadcast([P, P]), ident_f32[:])
+
+        def stats_hp():
+            nc.vector.bn_stats(out=hp_stats[:], in_=bank["hp"][:])
+
+        def aggregate_hp():
+            nc.vector.bn_aggr(out=hp_mean_var[:], in_=hp_stats[:])
+
+        def take_features(half):
+            chunks = slice(half * CHUNKS // 2, (half + 1) * CHUNKS // 2)
+            nc.scalar.copy(out=hpT[:, chunks, :], in_=bank["hpT"][:, chunks, :])
+
+        def scale_features_scalar(c):
             nc.scalar.mul(out=hpT_g[:, c, :], in_=hpT[:, c, :], mul=g_cols[:, c : c + 1])
-        hp_mean_var = keep.tile([P, 2], F32)
-        nc.vector.bn_aggr(out=hp_mean_var[:], in_=hp_stats[:])
-        for c in range(CHUNKS // 2, CHUNKS):
+
+        def scale_features_vector(c):
             nc.vector.tensor_scalar(
                 out=hpT_g[:, c, :], in0=hpT[:, c, :], scalar1=g_cols[:, c : c + 1], scalar2=None,
                 op0=ALU.mult,
             )
-        sum_all_ps = psum.tile([P, P], F32, tag="small")
-        nc.tensor.transpose(sum_all_ps[:], hp_sum[:].to_broadcast([P, P]), ident_f32[:])
-        hpT_hat_g = keep.tile([P, CHUNKS, P], F32)
-        for c in range(CHUNKS):
+
+        def centre_features(c):
             nc.vector.scalar_tensor_tensor(
-                out=hpT_hat_g[:, c, :], in0=sum_all_ps[:], scalar=neg_g_cols[:, c : c + 1],
+                out=hpT_hat_g[:, c, :], in0=bank["sum_all"][:], scalar=neg_g_cols[:, c : c + 1],
                 in1=hpT_g[:, c, :], op0=ALU.mult, op1=ALU.add,
             )
 
-        for c in range(CHUNKS):
-            nc.tensor.matmul(
-                var_ps[:], hpT[:, c, :], c_hat_2[:, :, c], start=False, stop=(c == CHUNKS - 1)
-            )
-        rstd = keep.tile([P, CODES], F32)
-        nc.scalar.activation(
-            out=rstd[:], in_=var_ps[:], func=ACT.Abs_reciprocal_sqrt, bias=hp_mean_var[:, 1:2],
-            scale=1.0,
-        )
-        nc.scalar.activation(out=table_warm[:, 1:2], in_=rstd[:, 0:1], func=ACT.Tanh)
-        nc.vector.quantize_mx(
-            out=w2_codes[:].bitcast(FP8X4),
-            scales=w2_scales[:],
-            in_=w2_grouped[:].rearrange("p n j -> p (n j)"),
-        )
+        def open_variances():
+            var_ps = open_bank("var", "b3", [P, CODES])
+            nc.tensor.matmul(var_ps[:], averager[:], c_sq_eps[:], start=True, stop=False)
 
-        mu_ln = keep.tile([P, CODES, CF], BF16)
-        ln_grouped = keep.tile([P, CODES, P * PACK], BF16, align_bytes=64)
-        ln_codes = keep.tile([P, CODES, P], U32, align_bytes=64)
-        ln_scales = keep.tile([P, CODES, P], U8, align_bytes=64)
-        out_banks = []
-        result = keep.tile([P, CODES, CF], F32)
-        free_banks = ("turn", "hp", "small", "vec")
+        def close_variances():
+            for c in range(CHUNKS):
+                nc.tensor.matmul(
+                    bank["var"][:], hpT[:, c, :], c_hat_2[:, :, c],
+                    start=False, stop=(c == CHUNKS - 1),
+                )
+
+        def take_root():
+            nc.scalar.activation(
+                out=rstd[:], in_=bank["var"][:], func=ACT.Abs_reciprocal_sqrt,
+                bias=hp_mean_var[:, 1:2], scale=1.0,
+            )
 
         def normalise(k):
             nc.vector.scalar_tensor_tensor(
-                out=mu_ln[:, k, :], in0=sum_ps[k][:], scalar=rstd[:, k : k + 1],
+                out=mu_ln[:, k, :], in0=bank["sum%d" % k][:], scalar=rstd[:, k : k + 1],
                 in1=b_all[:], op0=ALU.mult, op1=ALU.add,
             )
 
         def turn(k):
             words = mu_ln[:, k, :].bitcast(F32)
-            lnT_ps = psum.tile([P, 2, P], F32, tag="code%d" % k, name="lnT_ps%d" % k)
+            lnT_ps = open_bank("lnT%d" % k, "b%d" % (4 + k), [P, 2, P])
             for u in range(2):
                 nc.tensor.transpose(lnT_ps[:, u, :], words[:, u : 2 * P : 2], ident_f32[:])
             nc.scalar.copy(
@@ -321,14 +322,15 @@ def tile_mixtureconfounderprior_pa_s_kernel(
                 in_=lnT_ps[:].rearrange("p u t -> p t u"),
             )
 
-        def quantise_and_multiply(k):
+        def quantise(k):
             nc.vector.quantize_mx(
                 out=ln_codes[:, k, :].bitcast(FP8X4),
                 scales=ln_scales[:, k, :],
                 in_=ln_grouped[:, k, :],
             )
-            out_ps = psum.tile([P, CF], F32, tag=free_banks[k], name="out_ps%d" % k)
-            out_banks.append(out_ps)
+
+        def multiply(k):
+            out_ps = open_bank("out%d" % k, "b%d" % k, [P, CF])
             nc.tensor.matmul_mx(
                 out=out_ps[:],
                 lhsT=ln_codes[:, k, :].bitcast(FP8X4),
@@ -339,36 +341,104 @@ def tile_mixtureconfounderprior_pa_s_kernel(
                 stop=True,
             )
 
-        def add_bias(k, cols):
+        def add_bias(k, cols=slice(0, CF)):
             nc.vector.tensor_tensor(
-                out=result[:, k, cols], in0=out_banks[k][:, cols], in1=b2_all[:, cols], op=ALU.add
+                out=result[:, k, cols], in0=bank["out%d" % k][:, cols], in1=b2_all[:, cols],
+                op=ALU.add,
             )
 
-        def finish(k, cols):
+        def finish(k, cols=slice(0, CF)):
             nc.scalar.activation(out=result[:, k, cols], in_=result[:, k, cols], func=ACT.Tanh)
             nc.sync.dma_start(out=out_rows[:, k, cols], in_=result[:, k, cols])
 
-        for k in range(CODES - 1):
-            close_sum(k)
+        nc.vector.memset(vec_rows[:], 0.0)
+        load_w1(0)
+        load_vector(nc.scalar, 0, code_mu.rearrange("k (c p) -> (k c) p", p=P))
+        load_vector(nc.sync, VEC_B1, mu_b1.rearrange("(c p) -> c p", p=P))
+        load_vector(nc.sync, VEC_G, ln_g.rearrange("(c p) -> c p", p=P))
+        nc.sync.dma_start(out=h_sb[:], in_=h_rows)
+        load_w1(1)
+        load_w2()
+        nc.sync.dma_start(out=b_all[:], in_=ln_b.partition_broadcast(P))
+        nc.sync.dma_start(out=b2_all[:], in_=mu_b2.partition_broadcast(P))
+
+        nc.vector.memset(ones[:], 1.0)
+        nc.scalar.activation(
+            out=table_warm[:, 0:1], in_=ones[:, 0:1], func=ACT.Abs_reciprocal_sqrt
+        )
+        make_identity(nc, ident_bf16[:])
+        make_identity(nc, ident_f32[:])
+        nc.gpsimd.memset(neg_averager[:], -1.0 / CF)
+        nc.gpsimd.memset(averager[:], 1.0 / CF)
+        open_bank("idle", "b3", [P, P])
+        keep_warm(3)
+
+        turn_vectors()
+        regroup_w1(0)
+        take_vectors()
+        turn_h()
+        centre_codes()
+        quantise_w1(0)
+        regroup_w1(1)
+        scale_codes()
+        prepare_variances()
+        quantise_h()
+        quantise_w1(1)
+        keep_warm(1)
+        open_sum(0)
+        multiply_tokens(0)
+        multiply_tokens(1)
+        multiply_features()
+
+        regroup_w2_scalar()
+        sum_hp()
+        regroup_w2_vector()
+        stats_hp()
+        open_sum(1)
+        open_variances()
+        spread_hp_sum()
+        open_sum(2)
+        for half in range(2):
+            take_features(half)
+        aggregate_hp()
+        for c in range(CHUNKS):
+            if c < CHUNKS // 2:
+                scale_features_scalar(c)
+            else:
+                scale_features_vector(c)
+        for c in range(CHUNKS):
+            centre_features(c)
+        close_variances()
+        take_root()
+        nc.scalar.activation(out=table_warm[:, 1:2], in_=rstd[:, 0:1], func=ACT.Tanh)
+        quantise_w2()
+        close_sum(0)
+        close_sum(1)
+        open_sum(3)
+        close_sum(2)
+
         normalise(0)
         turn(0)
-        close_sum(CODES - 1)
+        close_sum(3)
         normalise(1)
         turn(1)
         normalise(2)
         turn(2)
+        quantise(0)
+        multiply(0)
         normalise(3)
-        quantise_and_multiply(0)
+        quantise(1)
+        multiply(1)
         turn(3)
-        quantise_and_multiply(1)
-        quantise_and_multiply(2)
-        whole = slice(0, CF)
-        add_bias(0, whole)
-        quantise_and_multiply(3)
-        finish(0, whole)
-        for k in range(1, CODES - 1):
-            add_bias(k, whole)
-            finish(k, whole)
+        add_bias(0)
+        quantise(2)
+        multiply(2)
+        add_bias(1)
+        quantise(3)
+        multiply(3)
+        add_bias(2)
+        for k in range(CODES - 1):
+            finish(k)
         for first in (0, CF // 2):
             add_bias(CODES - 1, slice(first, first + CF // 2))
             finish(CODES - 1, slice(first, first + CF // 2))

@@ -10,6 +10,7 @@ U8 = mybir.dt.uint8
 FP8X4 = mybir.dt.float8_e4m3fn_x4
 ALU = mybir.AluOpType
 ACT = mybir.ActivationFunctionType
+AXIS = mybir.AxisListType
 
 P = 128
 PACK = 4
@@ -68,7 +69,6 @@ def tile_mixtureconfounderprior_pa_s_kernel(
         c_hat_g = keep.tile(by_code, F32)
         c_hat_2 = keep.tile(by_code, F32)
         c_hat_sq = keep.tile(by_code, F32)
-        c_sq_pairs = keep.tile([P, CODES, 2], F32)
         c_sq_sum = keep.tile([P, CODES], F32)
         c_sq_eps = keep.tile([P, CODES], F32)
         h_grouped = keep.tile([P, PASSES1 * P * PACK], BF16, align_bytes=64)
@@ -115,6 +115,20 @@ def tile_mixtureconfounderprior_pa_s_kernel(
         def keep_warm(times):
             for i in range(times):
                 nc.tensor.matmul(bank["idle"][:], ones[:], ones[:], start=True, stop=True)
+
+        def keep_warm_mx(times):
+            if "idle_mx" not in bank:
+                open_bank("idle_mx", "b2", [P, CF])
+            for i in range(times):
+                nc.tensor.matmul_mx(
+                    out=bank["idle_mx"][:],
+                    lhsT=h_codes[:, 0:P].bitcast(FP8X4),
+                    lhsT_scale=h_scales[:, 0:P],
+                    rhs=w1_codes[:, 0, :].bitcast(FP8X4),
+                    rhs_scale=w1_scales[:, 0, :],
+                    start=True,
+                    stop=True,
+                )
 
         def turn_h():
             h_words = h_sb[:].bitcast(F32)
@@ -181,15 +195,11 @@ def tile_mixtureconfounderprior_pa_s_kernel(
         def prepare_variances():
             nc.scalar.mul(out=c_hat_2[:], in_=bank["c_hat"][:], mul=2.0 / CF)
             nc.scalar.activation(out=c_hat_sq[:], in_=bank["c_hat"][:], func=ACT.Square)
-            nc.gpsimd.tensor_tensor(
-                out=c_sq_pairs[:], in0=c_hat_sq[:, :, 0:2], in1=c_hat_sq[:, :, 2:4], op=ALU.add
-            )
-            nc.gpsimd.tensor_tensor(
-                out=c_sq_sum[:], in0=c_sq_pairs[:, :, 0], in1=c_sq_pairs[:, :, 1], op=ALU.add
-            )
-            nc.gpsimd.tensor_scalar(
-                out=c_sq_eps[:], in0=c_sq_sum[:], scalar1=CHUNKS * LN_EPS, scalar2=1.0,
-                op0=ALU.add, op1=ALU.mult,
+
+        def sum_squares():
+            nc.vector.tensor_reduce(out=c_sq_sum[:], in_=c_hat_sq[:], axis=AXIS.X, op=ALU.add)
+            nc.vector.tensor_scalar(
+                out=c_sq_eps[:], in0=c_sq_sum[:], scalar1=CHUNKS * LN_EPS, scalar2=None, op0=ALU.add
             )
 
         def open_sum(k):
@@ -317,6 +327,9 @@ def tile_mixtureconfounderprior_pa_s_kernel(
             lnT_ps = open_bank("lnT%d" % k, "b%d" % (4 + k), [P, 2, P])
             for u in range(2):
                 nc.tensor.transpose(lnT_ps[:, u, :], words[:, u : 2 * P : 2], ident_f32[:])
+
+        def take_turned(k):
+            lnT_ps = bank["lnT%d" % k]
             nc.scalar.copy(
                 out=ln_grouped[:, k, :].bitcast(F32).rearrange("p (t u) -> p t u", u=2),
                 in_=lnT_ps[:].rearrange("p u t -> p t u"),
@@ -371,21 +384,23 @@ def tile_mixtureconfounderprior_pa_s_kernel(
         nc.gpsimd.memset(neg_averager[:], -1.0 / CF)
         nc.gpsimd.memset(averager[:], 1.0 / CF)
         open_bank("idle", "b3", [P, P])
-        keep_warm(3)
+        keep_warm(4)
 
         turn_vectors()
         regroup_w1(0)
         take_vectors()
         turn_h()
         centre_codes()
+        keep_warm(2)
         quantise_w1(0)
-        regroup_w1(1)
         scale_codes()
+        regroup_w1(1)
         prepare_variances()
+        open_sum(0)
+        open_sum(1)
+        open_sum(2)
         quantise_h()
         quantise_w1(1)
-        keep_warm(1)
-        open_sum(0)
         multiply_tokens(0)
         multiply_tokens(1)
         multiply_features()
@@ -393,11 +408,11 @@ def tile_mixtureconfounderprior_pa_s_kernel(
         regroup_w2_scalar()
         sum_hp()
         regroup_w2_vector()
+        sum_squares()
         stats_hp()
-        open_sum(1)
-        open_variances()
+        open_sum(3)
         spread_hp_sum()
-        open_sum(2)
+        open_variances()
         for half in range(2):
             take_features(half)
         aggregate_hp()
@@ -414,16 +429,19 @@ def tile_mixtureconfounderprior_pa_s_kernel(
         quantise_w2()
         close_sum(0)
         close_sum(1)
-        open_sum(3)
+        keep_warm_mx(2)
         close_sum(2)
 
         normalise(0)
         turn(0)
+        take_turned(0)
         close_sum(3)
         normalise(1)
         turn(1)
+        take_turned(1)
         normalise(2)
         turn(2)
+        take_turned(2)
         quantise(0)
         multiply(0)
         normalise(3)
@@ -431,14 +449,16 @@ def tile_mixtureconfounderprior_pa_s_kernel(
         multiply(1)
         turn(3)
         add_bias(0)
+        finish(0)
+        take_turned(3)
         quantise(2)
         multiply(2)
         add_bias(1)
+        finish(1)
         quantise(3)
         multiply(3)
         add_bias(2)
-        for k in range(CODES - 1):
-            finish(k)
+        finish(2)
         for first in (0, CF // 2):
             add_bias(CODES - 1, slice(first, first + CF // 2))
             finish(CODES - 1, slice(first, first + CF // 2))

@@ -116,12 +116,11 @@ def tile_mixtureconfounderprior_pa_s_kernel(
             for i in range(times):
                 nc.tensor.matmul(bank["idle"][:], ones[:], ones[:], start=True, stop=True)
 
-        def keep_warm_mx(times):
-            if "idle_mx" not in bank:
-                open_bank("idle_mx", "b2", [P, CF])
+        def keep_warm_mx(tag, times):
+            idle_ps = open_bank("idle_" + tag, tag, [P, CF])
             for i in range(times):
                 nc.tensor.matmul_mx(
-                    out=bank["idle_mx"][:],
+                    out=idle_ps[:],
                     lhsT=h_codes[:, 0:P].bitcast(FP8X4),
                     lhsT_scale=h_scales[:, 0:P],
                     rhs=w1_codes[:, 0, :].bitcast(FP8X4),
@@ -384,33 +383,37 @@ def tile_mixtureconfounderprior_pa_s_kernel(
         nc.gpsimd.memset(neg_averager[:], -1.0 / CF)
         nc.gpsimd.memset(averager[:], 1.0 / CF)
         open_bank("idle", "b3", [P, P])
-        keep_warm(4)
+        keep_warm(3)
 
+        keep_warm(1)
         turn_vectors()
+        keep_warm(1)
         regroup_w1(0)
         take_vectors()
         turn_h()
         centre_codes()
-        keep_warm(2)
         quantise_w1(0)
         scale_codes()
         regroup_w1(1)
         prepare_variances()
+        keep_warm(1)
         open_sum(0)
+        keep_warm(1)
         open_sum(1)
+        keep_warm(1)
         open_sum(2)
         quantise_h()
         quantise_w1(1)
         multiply_tokens(0)
         multiply_tokens(1)
         multiply_features()
+        keep_warm_mx("b7", 2)
 
         regroup_w2_scalar()
         sum_hp()
         regroup_w2_vector()
         sum_squares()
         stats_hp()
-        open_sum(3)
         spread_hp_sum()
         open_variances()
         for half in range(2):
@@ -429,16 +432,19 @@ def tile_mixtureconfounderprior_pa_s_kernel(
         quantise_w2()
         close_sum(0)
         close_sum(1)
-        keep_warm_mx(2)
+        keep_warm_mx("b1", 1)
+        open_sum(3)
         close_sum(2)
 
         normalise(0)
         turn(0)
         take_turned(0)
         close_sum(3)
+        keep_warm_mx("b1", 1)
         normalise(1)
         turn(1)
         take_turned(1)
+        keep_warm_mx("b1", 1)
         normalise(2)
         turn(2)
         take_turned(2)
@@ -448,17 +454,16 @@ def tile_mixtureconfounderprior_pa_s_kernel(
         quantise(1)
         multiply(1)
         turn(3)
-        add_bias(0)
-        finish(0)
         take_turned(3)
+        add_bias(0)
         quantise(2)
         multiply(2)
         add_bias(1)
-        finish(1)
         quantise(3)
         multiply(3)
         add_bias(2)
-        finish(2)
+        for k in range(CODES - 1):
+            finish(k)
         for first in (0, CF // 2):
             add_bias(CODES - 1, slice(first, first + CF // 2))
             finish(CODES - 1, slice(first, first + CF // 2))

@@ -19,13 +19,15 @@ PASSES1 = D // (P * PACK)
 CODES = 4
 CF = 512
 CHUNKS = CF // P
+HALVES = 2
+HALF = CF // HALVES
 LN_EPS = 1e-5
 
 VEC_B1, VEC_G = 4, 5
 VECTORS = 6
 VEC_ROWS = VECTORS * CHUNKS
 
-W1_VECTOR = (352, 352)
+W1_VECTOR = (352, 384)
 W2_VECTOR = 224
 
 FLOPS = 2 * P * D * CF + 2 * P * CODES * CF * CF
@@ -81,8 +83,8 @@ def tile_mixtureconfounderprior_pa_s_kernel(
         w2_codes = keep.tile([P, CF], U32, align_bytes=64)
         w2_scales = keep.tile([P, CF], U8, align_bytes=64)
         unread = keep.tile([P, CF], BF16)
-        hp_sum = keep.tile([P, 1], F32)
-        hp_stats = keep.tile([P, 6], F32)
+        hp_sum = keep.tile([P, HALVES], F32)
+        hp_stats = keep.tile([P, HALVES, 6], F32)
         hp_mean_var = keep.tile([P, 2], F32)
         hpT = keep.tile([P, CHUNKS, P], F32)
         hpT_g = keep.tile([P, CHUNKS, P], F32)
@@ -116,13 +118,18 @@ def tile_mixtureconfounderprior_pa_s_kernel(
             for i in range(times):
                 nc.tensor.matmul(bank["idle"][:], ones[:], ones[:], start=True, stop=True)
 
+        def keep_warm2(tag, times):
+            idle_ps = open_bank("idle_" + tag, tag, [P, P])
+            for i in range(times):
+                nc.tensor.matmul(idle_ps[:], ones[:], ones[:], start=True, stop=True)
+
         def keep_warm_mx(tag, times):
             idle_ps = open_bank("idle_" + tag, tag, [P, CF])
             for i in range(times):
                 nc.tensor.matmul_mx(
                     out=idle_ps[:],
-                    lhsT=h_codes[:, 0:P].bitcast(FP8X4),
-                    lhsT_scale=h_scales[:, 0:P],
+                    lhsT=w1_codes[:, 0, 0:P].bitcast(FP8X4),
+                    lhsT_scale=w1_scales[:, 0, 0:P],
                     rhs=w1_codes[:, 0, :].bitcast(FP8X4),
                     rhs_scale=w1_scales[:, 0, :],
                     start=True,
@@ -225,17 +232,19 @@ def tile_mixtureconfounderprior_pa_s_kernel(
                 )
 
         def multiply_tokens(g):
-            if g == 0:
-                open_bank("hp", "b1", [P, CF])
-            nc.tensor.matmul_mx(
-                out=bank["hp"][:],
-                lhsT=h_codes[:, g * P : (g + 1) * P].bitcast(FP8X4),
-                lhsT_scale=h_scales[:, g * P : (g + 1) * P],
-                rhs=w1_codes[:, g, :].bitcast(FP8X4),
-                rhs_scale=w1_scales[:, g, :],
-                start=(g == 0),
-                stop=(g == PASSES1 - 1),
-            )
+            for half in range(HALVES):
+                if g == 0:
+                    open_bank("hp%d" % half, ("b1", "b3")[half], [P, HALF])
+                cols = slice(half * HALF, (half + 1) * HALF)
+                nc.tensor.matmul_mx(
+                    out=bank["hp%d" % half][:],
+                    lhsT=h_codes[:, g * P : (g + 1) * P].bitcast(FP8X4),
+                    lhsT_scale=h_scales[:, g * P : (g + 1) * P],
+                    rhs=w1_codes[:, g, cols].bitcast(FP8X4),
+                    rhs_scale=w1_scales[:, g, cols],
+                    start=(g == 0),
+                    stop=(g == PASSES1 - 1),
+                )
 
         def multiply_features():
             hpT_ps = open_bank("hpT", "b0", [P, CHUNKS, P])
@@ -266,18 +275,30 @@ def tile_mixtureconfounderprior_pa_s_kernel(
 
         def sum_hp():
             nc.scalar.activation(
-                out=unread[:], in_=bank["hp"][:], func=ACT.Identity, accum_out=hp_sum[:]
+                out=unread[:, 0:HALF], in_=bank["hp0"][:], func=ACT.Identity,
+                accum_out=hp_sum[:, 0:1],
             )
+            nc.vector.tensor_reduce(out=hp_sum[:, 1:2], in_=bank["hp1"][:], axis=AXIS.X, op=ALU.add)
 
         def spread_hp_sum():
             sum_all_ps = open_bank("sum_all", "b2", [P, P])
-            nc.tensor.transpose(sum_all_ps[:], hp_sum[:].to_broadcast([P, P]), ident_f32[:])
+            for half in (1, 0):
+                nc.tensor.matmul(
+                    sum_all_ps[:],
+                    hp_sum[:, half : half + 1].to_broadcast([P, P]),
+                    ident_f32[:],
+                    start=(half == 1),
+                    stop=(half == 0),
+                    is_transpose=True,
+                )
 
-        def stats_hp():
-            nc.vector.bn_stats(out=hp_stats[:], in_=bank["hp"][:])
+        def stats_hp(half):
+            nc.vector.bn_stats(out=hp_stats[:, half, :], in_=bank["hp%d" % half][:])
 
         def aggregate_hp():
-            nc.vector.bn_aggr(out=hp_mean_var[:], in_=hp_stats[:])
+            nc.vector.bn_aggr(
+                out=hp_mean_var[:], in_=hp_stats[:].rearrange("p h s -> p (h s)")
+            )
 
         def take_features(half):
             chunks = slice(half * CHUNKS // 2, (half + 1) * CHUNKS // 2)
@@ -299,7 +320,7 @@ def tile_mixtureconfounderprior_pa_s_kernel(
             )
 
         def open_variances():
-            var_ps = open_bank("var", "b3", [P, CODES])
+            var_ps = open_bank("var", "b1", [P, CODES])
             nc.tensor.matmul(var_ps[:], averager[:], c_sq_eps[:], start=True, stop=False)
 
         def close_variances():
@@ -315,17 +336,21 @@ def tile_mixtureconfounderprior_pa_s_kernel(
                 bias=hp_mean_var[:, 1:2], scale=1.0,
             )
 
-        def normalise(k):
-            nc.vector.scalar_tensor_tensor(
-                out=mu_ln[:, k, :], in0=bank["sum%d" % k][:], scalar=rstd[:, k : k + 1],
-                in1=b_all[:], op0=ALU.mult, op1=ALU.add,
-            )
+        def normalise(k, parts=None):
+            for u in (range(2) if parts is None else (parts,)):
+                nc.vector.scalar_tensor_tensor(
+                    out=mu_ln[:, k, u * 2 * P : (u + 1) * 2 * P].rearrange("t (p e) -> t p e", e=2),
+                    in0=bank["sum%d" % k][:].rearrange("t (p u e) -> t u p e", u=2, e=2)[:, u],
+                    scalar=rstd[:, k : k + 1],
+                    in1=b_all[:].rearrange("t (p u e) -> t u p e", u=2, e=2)[:, u],
+                    op0=ALU.mult, op1=ALU.add,
+                )
 
         def turn(k):
             words = mu_ln[:, k, :].bitcast(F32)
             lnT_ps = open_bank("lnT%d" % k, "b%d" % (4 + k), [P, 2, P])
             for u in range(2):
-                nc.tensor.transpose(lnT_ps[:, u, :], words[:, u : 2 * P : 2], ident_f32[:])
+                nc.tensor.transpose(lnT_ps[:, u, :], words[:, u * P : (u + 1) * P], ident_f32[:])
 
         def take_turned(k):
             lnT_ps = bank["lnT%d" % k]
@@ -363,11 +388,11 @@ def tile_mixtureconfounderprior_pa_s_kernel(
             nc.scalar.activation(out=result[:, k, cols], in_=result[:, k, cols], func=ACT.Tanh)
             nc.sync.dma_start(out=out_rows[:, k, cols], in_=result[:, k, cols])
 
-        nc.vector.memset(vec_rows[:], 0.0)
-        load_w1(0)
+        nc.gpsimd.memset(vec_rows[:], 0.0)
         load_vector(nc.scalar, 0, code_mu.rearrange("k (c p) -> (k c) p", p=P))
-        load_vector(nc.sync, VEC_B1, mu_b1.rearrange("(c p) -> c p", p=P))
-        load_vector(nc.sync, VEC_G, ln_g.rearrange("(c p) -> c p", p=P))
+        load_vector(nc.scalar, VEC_B1, mu_b1.rearrange("(c p) -> c p", p=P))
+        load_vector(nc.scalar, VEC_G, ln_g.rearrange("(c p) -> c p", p=P))
+        load_w1(0)
         nc.sync.dma_start(out=h_sb[:], in_=h_rows)
         load_w1(1)
         load_w2()
@@ -383,84 +408,82 @@ def tile_mixtureconfounderprior_pa_s_kernel(
         nc.gpsimd.memset(neg_averager[:], -1.0 / CF)
         nc.gpsimd.memset(averager[:], 1.0 / CF)
         open_bank("idle", "b3", [P, P])
-        keep_warm(3)
-
-        keep_warm(1)
         turn_vectors()
-        keep_warm(1)
-        regroup_w1(0)
         take_vectors()
-        turn_h()
         centre_codes()
-        quantise_w1(0)
-        scale_codes()
-        regroup_w1(1)
+        regroup_w1(0)
         prepare_variances()
+        scale_codes()
+        quantise_w1(0)
+        keep_warm(2)
+        turn_h()
         keep_warm(1)
         open_sum(0)
-        keep_warm(1)
         open_sum(1)
         keep_warm(1)
         open_sum(2)
+        open_sum(3)
+        regroup_w1(1)
         quantise_h()
         quantise_w1(1)
+        keep_warm_mx("b2", 2)
         multiply_tokens(0)
         multiply_tokens(1)
         multiply_features()
-        keep_warm_mx("b7", 2)
+        keep_warm_mx("b2", 1)
 
         regroup_w2_scalar()
-        sum_hp()
         regroup_w2_vector()
         sum_squares()
-        stats_hp()
+        sum_hp()
+        stats_hp(0)
+        stats_hp(1)
         spread_hp_sum()
+        keep_warm_mx("b1", 1)
         open_variances()
         for half in range(2):
             take_features(half)
-        aggregate_hp()
         for c in range(CHUNKS):
-            if c < CHUNKS // 2:
-                scale_features_scalar(c)
-            else:
-                scale_features_vector(c)
+            scale_features_vector(c)
         for c in range(CHUNKS):
             centre_features(c)
+        aggregate_hp()
         close_variances()
+        keep_warm2("b3", 1)
         take_root()
         nc.scalar.activation(out=table_warm[:, 1:2], in_=rstd[:, 0:1], func=ACT.Tanh)
         quantise_w2()
         close_sum(0)
+        keep_warm2("b3", 1)
         close_sum(1)
-        keep_warm_mx("b1", 1)
-        open_sum(3)
         close_sum(2)
-
+        close_sum(3)
         normalise(0)
         turn(0)
         take_turned(0)
-        close_sum(3)
-        keep_warm_mx("b1", 1)
+        keep_warm2("b3", 1)
         normalise(1)
         turn(1)
         take_turned(1)
-        keep_warm_mx("b1", 1)
+        keep_warm2("b3", 1)
         normalise(2)
         turn(2)
         take_turned(2)
+        normalise(3, 0)
         quantise(0)
+        normalise(3, 1)
         multiply(0)
-        normalise(3)
-        quantise(1)
-        multiply(1)
         turn(3)
         take_turned(3)
+        quantise(1)
+        multiply(1)
+        keep_warm_mx("b3", 2)
         add_bias(0)
         quantise(2)
         multiply(2)
-        add_bias(1)
         quantise(3)
         multiply(3)
+        add_bias(1)
         add_bias(2)
         for k in range(CODES - 1):
             finish(k)

@@ -389,9 +389,9 @@ def tile_mixtureconfounderprior_pa_s_kernel(
             nc.sync.dma_start(out=out_rows[:, k, cols], in_=result[:, k, cols])
 
         nc.gpsimd.memset(vec_rows[:], 0.0)
-        load_vector(nc.scalar, 0, code_mu.rearrange("k (c p) -> (k c) p", p=P))
-        load_vector(nc.scalar, VEC_B1, mu_b1.rearrange("(c p) -> c p", p=P))
-        load_vector(nc.scalar, VEC_G, ln_g.rearrange("(c p) -> c p", p=P))
+        load_vector(nc.sync, 0, code_mu.rearrange("k (c p) -> (k c) p", p=P))
+        load_vector(nc.sync, VEC_B1, mu_b1.rearrange("(c p) -> c p", p=P))
+        load_vector(nc.sync, VEC_G, ln_g.rearrange("(c p) -> c p", p=P))
         load_w1(0)
         nc.sync.dma_start(out=h_sb[:], in_=h_rows)
         load_w1(1)
@@ -408,14 +408,16 @@ def tile_mixtureconfounderprior_pa_s_kernel(
         nc.gpsimd.memset(neg_averager[:], -1.0 / CF)
         nc.gpsimd.memset(averager[:], 1.0 / CF)
         open_bank("idle", "b3", [P, P])
+        keep_warm(3)
         turn_vectors()
         take_vectors()
+        keep_warm(1)
         centre_codes()
         regroup_w1(0)
         prepare_variances()
         scale_codes()
         quantise_w1(0)
-        keep_warm(2)
+        keep_warm(1)
         turn_h()
         keep_warm(1)
         open_sum(0)
@@ -426,7 +428,7 @@ def tile_mixtureconfounderprior_pa_s_kernel(
         regroup_w1(1)
         quantise_h()
         quantise_w1(1)
-        keep_warm_mx("b2", 2)
+        keep_warm_mx("b2", 1)
         multiply_tokens(0)
         multiply_tokens(1)
         multiply_features()
@@ -449,23 +451,23 @@ def tile_mixtureconfounderprior_pa_s_kernel(
             centre_features(c)
         aggregate_hp()
         close_variances()
-        keep_warm2("b3", 1)
+        keep_warm_mx("b3", 1)
         take_root()
         nc.scalar.activation(out=table_warm[:, 1:2], in_=rstd[:, 0:1], func=ACT.Tanh)
         quantise_w2()
         close_sum(0)
-        keep_warm2("b3", 1)
         close_sum(1)
+        keep_warm_mx("b3", 1)
         close_sum(2)
-        close_sum(3)
         normalise(0)
         turn(0)
         take_turned(0)
+        close_sum(3)
         keep_warm2("b3", 1)
         normalise(1)
         turn(1)
         take_turned(1)
-        keep_warm2("b3", 1)
+        keep_warm_mx("b3", 1)
         normalise(2)
         turn(2)
         take_turned(2)

@@ -21,13 +21,14 @@ CF = 512
 CHUNKS = CF // P
 HALVES = 2
 HALF = CF // HALVES
+REPEATS = 16
 LN_EPS = 1e-5
 
 VEC_B1, VEC_G = 4, 5
 VECTORS = 6
 VEC_ROWS = VECTORS * CHUNKS
 
-W1_VECTOR = (352, 384)
+W1_VECTOR = (352, 352)
 W2_VECTOR = 224
 
 FLOPS = 2 * P * D * CF + 2 * P * CODES * CF * CF
@@ -68,6 +69,7 @@ def tile_mixtureconfounderprior_pa_s_kernel(
         g_cols = keep.tile([P, CHUNKS], F32)
         neg_g_cols = keep.tile([P, CHUNKS], F32)
         by_code = [P, CODES, CHUNKS]
+        by_rep = [P, CODES, REPEATS]
         c_hat_g = keep.tile(by_code, F32)
         c_hat_2 = keep.tile(by_code, F32)
         c_hat_sq = keep.tile(by_code, F32)
@@ -119,19 +121,17 @@ def tile_mixtureconfounderprior_pa_s_kernel(
                 nc.tensor.matmul(bank["idle"][:], ones[:], ones[:], start=True, stop=True)
 
         def keep_warm2(tag, times):
-            idle_ps = open_bank("idle_" + tag, tag, [P, P])
             for i in range(times):
-                nc.tensor.matmul(idle_ps[:], ones[:], ones[:], start=True, stop=True)
+                nc.tensor.matmul(bank[tag][:, 0:P], ones[:], ones[:], start=True, stop=True)
 
         def keep_warm_mx(tag, times):
-            idle_ps = open_bank("idle_" + tag, tag, [P, CF])
             for i in range(times):
                 nc.tensor.matmul_mx(
-                    out=idle_ps[:],
+                    out=bank[tag][:, 0:HALF],
                     lhsT=w1_codes[:, 0, 0:P].bitcast(FP8X4),
                     lhsT_scale=w1_scales[:, 0, 0:P],
-                    rhs=w1_codes[:, 0, :].bitcast(FP8X4),
-                    rhs_scale=w1_scales[:, 0, :],
+                    rhs=w1_codes[:, 0, 0:HALF].bitcast(FP8X4),
+                    rhs_scale=w1_scales[:, 0, 0:HALF],
                     start=True,
                     stop=True,
                 )
@@ -158,11 +158,11 @@ def tile_mixtureconfounderprior_pa_s_kernel(
             regroup(nc.vector.tensor_copy, w1_grouped[:, g, :cut], w1_rows[:, g, :, :cut])
             regroup(nc.scalar.copy, w1_grouped[:, g, cut:], w1_rows[:, g, :, cut:])
 
-        def quantise_w1(g):
+        def quantise_w1(g, cols=slice(0, CF)):
             nc.vector.quantize_mx(
-                out=w1_codes[:, g, :].bitcast(FP8X4),
-                scales=w1_scales[:, g, :],
-                in_=w1_grouped[:, g].rearrange("p n j -> p (n j)"),
+                out=w1_codes[:, g, cols].bitcast(FP8X4),
+                scales=w1_scales[:, g, cols],
+                in_=w1_grouped[:, g, cols].rearrange("p n j -> p (n j)"),
             )
 
         def turn_vectors():
@@ -204,6 +204,8 @@ def tile_mixtureconfounderprior_pa_s_kernel(
 
         def sum_squares():
             nc.vector.tensor_reduce(out=c_sq_sum[:], in_=c_hat_sq[:], axis=AXIS.X, op=ALU.add)
+
+        def add_eps():
             nc.vector.tensor_scalar(
                 out=c_sq_eps[:], in0=c_sq_sum[:], scalar1=CHUNKS * LN_EPS, scalar2=None, op0=ALU.add
             )
@@ -231,11 +233,11 @@ def tile_mixtureconfounderprior_pa_s_kernel(
                     is_transpose=True,
                 )
 
-        def multiply_tokens(g):
-            for half in range(HALVES):
+        def multiply_tokens(half, passes=range(PASSES1)):
+            cols = slice(half * HALF, (half + 1) * HALF)
+            for g in passes:
                 if g == 0:
-                    open_bank("hp%d" % half, ("b1", "b3")[half], [P, HALF])
-                cols = slice(half * HALF, (half + 1) * HALF)
+                    open_bank("hp%d" % half, ("b1", "b7")[half], [P, HALF])
                 nc.tensor.matmul_mx(
                     out=bank["hp%d" % half][:],
                     lhsT=h_codes[:, g * P : (g + 1) * P].bitcast(FP8X4),
@@ -246,12 +248,13 @@ def tile_mixtureconfounderprior_pa_s_kernel(
                     stop=(g == PASSES1 - 1),
                 )
 
-        def multiply_features():
-            hpT_ps = open_bank("hpT", "b0", [P, CHUNKS, P])
-            for c in range(CHUNKS):
+        def multiply_features(half):
+            if half == 0:
+                open_bank("hpT", "b0", [P, CHUNKS, P])
+            for c in range(half * CHUNKS // 2, (half + 1) * CHUNKS // 2):
                 for g in range(PASSES1):
                     nc.tensor.matmul_mx(
-                        out=hpT_ps[:, c, :],
+                        out=bank["hpT"][:, c, :],
                         lhsT=w1_codes[:, g, c * P : (c + 1) * P].bitcast(FP8X4),
                         lhsT_scale=w1_scales[:, g, c * P : (c + 1) * P],
                         rhs=h_codes[:, g * P : (g + 1) * P].bitcast(FP8X4),
@@ -278,6 +281,8 @@ def tile_mixtureconfounderprior_pa_s_kernel(
                 out=unread[:, 0:HALF], in_=bank["hp0"][:], func=ACT.Identity,
                 accum_out=hp_sum[:, 0:1],
             )
+
+        def sum_hp1():
             nc.vector.tensor_reduce(out=hp_sum[:, 1:2], in_=bank["hp1"][:], axis=AXIS.X, op=ALU.add)
 
         def spread_hp_sum():
@@ -320,19 +325,21 @@ def tile_mixtureconfounderprior_pa_s_kernel(
             )
 
         def open_variances():
-            var_ps = open_bank("var", "b1", [P, CODES])
-            nc.tensor.matmul(var_ps[:], averager[:], c_sq_eps[:], start=True, stop=False)
+            var_ps = open_bank("var", "b3", by_rep)
+            nc.tensor.matmul(
+                var_ps[:], averager[:], c_sq_eps[:].unsqueeze(2).to_broadcast(by_rep), start=True, stop=False
+            )
 
-        def close_variances():
-            for c in range(CHUNKS):
+        def close_variances(half):
+            for c in range(half * CHUNKS // 2, (half + 1) * CHUNKS // 2):
                 nc.tensor.matmul(
-                    bank["var"][:], hpT[:, c, :], c_hat_2[:, :, c],
+                    bank["var"][:], hpT[:, c, :], c_hat_2[:, :, c : c + 1].to_broadcast(by_rep),
                     start=False, stop=(c == CHUNKS - 1),
                 )
 
         def take_root():
             nc.scalar.activation(
-                out=rstd[:], in_=bank["var"][:], func=ACT.Abs_reciprocal_sqrt,
+                out=rstd[:], in_=bank["var"][:, :, 0], func=ACT.Abs_reciprocal_sqrt,
                 bias=hp_mean_var[:, 1:2], scale=1.0,
             )
 
@@ -388,10 +395,14 @@ def tile_mixtureconfounderprior_pa_s_kernel(
             nc.scalar.activation(out=result[:, k, cols], in_=result[:, k, cols], func=ACT.Tanh)
             nc.sync.dma_start(out=out_rows[:, k, cols], in_=result[:, k, cols])
 
-        nc.gpsimd.memset(vec_rows[:], 0.0)
-        load_vector(nc.sync, 0, code_mu.rearrange("k (c p) -> (k c) p", p=P))
-        load_vector(nc.sync, VEC_B1, mu_b1.rearrange("(c p) -> c p", p=P))
+        code_rows = code_mu.rearrange("k (c p) -> (k c) p", p=P)
+        load_vector(nc.scalar, 0, code_rows)
+        load_vector(nc.scalar, VEC_B1, mu_b1.rearrange("(c p) -> c p", p=P))
         load_vector(nc.sync, VEC_G, ln_g.rearrange("(c p) -> c p", p=P))
+        load_vector(nc.sync, VECTORS, code_rows[0 : 32 - VEC_ROWS, :])
+        nc.vector.memset(ones[:], 1.0)
+        nc.vector.memset(vec_rows[32:64, :], 0.0)
+        nc.vector.memset(vec_rows[64:128, :], 0.0)
         load_w1(0)
         nc.sync.dma_start(out=h_sb[:], in_=h_rows)
         load_w1(1)
@@ -399,7 +410,6 @@ def tile_mixtureconfounderprior_pa_s_kernel(
         nc.sync.dma_start(out=b_all[:], in_=ln_b.partition_broadcast(P))
         nc.sync.dma_start(out=b2_all[:], in_=mu_b2.partition_broadcast(P))
 
-        nc.vector.memset(ones[:], 1.0)
         nc.scalar.activation(
             out=table_warm[:, 0:1], in_=ones[:, 0:1], func=ACT.Abs_reciprocal_sqrt
         )
@@ -416,73 +426,67 @@ def tile_mixtureconfounderprior_pa_s_kernel(
         regroup_w1(0)
         prepare_variances()
         scale_codes()
+        sum_squares()
         quantise_w1(0)
+        add_eps()
         keep_warm(1)
         turn_h()
-        keep_warm(1)
         open_sum(0)
         open_sum(1)
-        keep_warm(1)
         open_sum(2)
-        open_sum(3)
+        open_variances()
         regroup_w1(1)
         quantise_h()
-        quantise_w1(1)
-        keep_warm_mx("b2", 1)
+        quantise_w1(1, slice(0, HALF))
+        quantise_w1(1, slice(HALF, CF))
         multiply_tokens(0)
         multiply_tokens(1)
-        multiply_features()
-        keep_warm_mx("b2", 1)
+        multiply_features(0)
+        multiply_features(1)
 
         regroup_w2_scalar()
         regroup_w2_vector()
-        sum_squares()
         sum_hp()
+        take_features(0)
+        take_features(1)
+        sum_hp1()
         stats_hp(0)
         stats_hp(1)
         spread_hp_sum()
-        keep_warm_mx("b1", 1)
-        open_variances()
-        for half in range(2):
-            take_features(half)
+        close_variances(0)
+        close_variances(1)
         for c in range(CHUNKS):
             scale_features_vector(c)
         for c in range(CHUNKS):
             centre_features(c)
         aggregate_hp()
-        close_variances()
-        keep_warm_mx("b3", 1)
         take_root()
         nc.scalar.activation(out=table_warm[:, 1:2], in_=rstd[:, 0:1], func=ACT.Tanh)
         quantise_w2()
         close_sum(0)
         close_sum(1)
-        keep_warm_mx("b3", 1)
         close_sum(2)
+        open_sum(3)
+        close_sum(3)
         normalise(0)
         turn(0)
         take_turned(0)
-        close_sum(3)
-        keep_warm2("b3", 1)
         normalise(1)
         turn(1)
         take_turned(1)
-        keep_warm_mx("b3", 1)
         normalise(2)
         turn(2)
         take_turned(2)
-        normalise(3, 0)
+        normalise(3)
         quantise(0)
-        normalise(3, 1)
-        multiply(0)
         turn(3)
+        multiply(0)
         take_turned(3)
         quantise(1)
         multiply(1)
-        keep_warm_mx("b3", 2)
-        add_bias(0)
         quantise(2)
         multiply(2)
+        add_bias(0)
         quantise(3)
         multiply(3)
         add_bias(1)

@@ -21,6 +21,7 @@ CF = 512
 CHUNKS = CF // P
 HALVES = 2
 HALF = CF // HALVES
+LEFT, RIGHT = slice(0, HALF), slice(HALF, CF)
 REPEATS = 16
 LN_EPS = 1e-5
 
@@ -28,8 +29,8 @@ VEC_B1, VEC_G = 4, 5
 VECTORS = 6
 VEC_ROWS = VECTORS * CHUNKS
 
-W1_VECTOR = (352, 352)
-W2_VECTOR = 224
+W1_VECTOR = 352
+W2_VECTOR = 256
 
 FLOPS = 2 * P * D * CF + 2 * P * CODES * CF * CF
 
@@ -153,10 +154,11 @@ def tile_mixtureconfounderprior_pa_s_kernel(
                 out=h_codes[:].bitcast(FP8X4), scales=h_scales[:], in_=h_grouped[:]
             )
 
-        def regroup_w1(g):
-            cut = W1_VECTOR[g]
-            regroup(nc.vector.tensor_copy, w1_grouped[:, g, :cut], w1_rows[:, g, :, :cut])
-            regroup(nc.scalar.copy, w1_grouped[:, g, cut:], w1_rows[:, g, :, cut:])
+        def regroup_w1_vector(g, cols):
+            regroup(nc.vector.tensor_copy, w1_grouped[:, g, cols], w1_rows[:, g, :, cols])
+
+        def regroup_w1_scalar(g, cols):
+            regroup(nc.scalar.copy, w1_grouped[:, g, cols], w1_rows[:, g, :, cols])
 
         def quantise_w1(g, cols=slice(0, CF)):
             nc.vector.quantize_mx(
@@ -287,13 +289,13 @@ def tile_mixtureconfounderprior_pa_s_kernel(
 
         def spread_hp_sum():
             sum_all_ps = open_bank("sum_all", "b2", [P, P])
-            for half in (1, 0):
+            for half in range(HALVES):
                 nc.tensor.matmul(
                     sum_all_ps[:],
                     hp_sum[:, half : half + 1].to_broadcast([P, P]),
                     ident_f32[:],
-                    start=(half == 1),
-                    stop=(half == 0),
+                    start=(half == 0),
+                    stop=(half == HALVES - 1),
                     is_transpose=True,
                 )
 
@@ -305,12 +307,13 @@ def tile_mixtureconfounderprior_pa_s_kernel(
                 out=hp_mean_var[:], in_=hp_stats[:].rearrange("p h s -> p (h s)")
             )
 
-        def take_features(half):
-            chunks = slice(half * CHUNKS // 2, (half + 1) * CHUNKS // 2)
-            nc.scalar.copy(out=hpT[:, chunks, :], in_=bank["hpT"][:, chunks, :])
+        def take_features(c):
+            nc.scalar.copy(out=hpT[:, c, :], in_=bank["hpT"][:, c, :])
 
         def scale_features_scalar(c):
-            nc.scalar.mul(out=hpT_g[:, c, :], in_=hpT[:, c, :], mul=g_cols[:, c : c + 1])
+            nc.scalar.mul(
+                out=hpT_g[:, c, :], in_=bank["hpT"][:, c, :], mul=g_cols[:, c : c + 1]
+            )
 
         def scale_features_vector(c):
             nc.vector.tensor_scalar(
@@ -391,8 +394,10 @@ def tile_mixtureconfounderprior_pa_s_kernel(
                 op=ALU.add,
             )
 
-        def finish(k, cols=slice(0, CF)):
+        def tanh(k, cols=slice(0, CF)):
             nc.scalar.activation(out=result[:, k, cols], in_=result[:, k, cols], func=ACT.Tanh)
+
+        def store(k, cols=slice(0, CF)):
             nc.sync.dma_start(out=out_rows[:, k, cols], in_=result[:, k, cols])
 
         code_rows = code_mu.rearrange("k (c p) -> (k c) p", p=P)
@@ -423,22 +428,26 @@ def tile_mixtureconfounderprior_pa_s_kernel(
         take_vectors()
         keep_warm(1)
         centre_codes()
-        regroup_w1(0)
-        prepare_variances()
+        regroup_w1_vector(0, LEFT)
+        regroup_w1_vector(0, slice(HALF, W1_VECTOR))
+        regroup_w1_scalar(0, slice(W1_VECTOR, CF))
         scale_codes()
+        prepare_variances()
+        quantise_w1(0, LEFT)
+        quantise_w1(0, RIGHT)
         sum_squares()
-        quantise_w1(0)
-        add_eps()
         keep_warm(1)
         turn_h()
         open_sum(0)
         open_sum(1)
         open_sum(2)
-        open_variances()
-        regroup_w1(1)
+        regroup_w1_vector(1, slice(0, W1_VECTOR))
+        regroup_w1_scalar(1, slice(W1_VECTOR, CF))
+        add_eps()
         quantise_h()
-        quantise_w1(1, slice(0, HALF))
-        quantise_w1(1, slice(HALF, CF))
+        quantise_w1(1, LEFT)
+        quantise_w1(1, RIGHT)
+        open_variances()
         multiply_tokens(0)
         multiply_tokens(1)
         multiply_features(0)
@@ -447,16 +456,19 @@ def tile_mixtureconfounderprior_pa_s_kernel(
         regroup_w2_scalar()
         regroup_w2_vector()
         sum_hp()
-        take_features(0)
-        take_features(1)
         sum_hp1()
-        stats_hp(0)
         stats_hp(1)
         spread_hp_sum()
+        for c in range(CHUNKS):
+            take_features(c)
         close_variances(0)
         close_variances(1)
         for c in range(CHUNKS):
-            scale_features_vector(c)
+            if c < CHUNKS // 2:
+                scale_features_vector(c)
+            else:
+                scale_features_scalar(c)
+        stats_hp(0)
         for c in range(CHUNKS):
             centre_features(c)
         aggregate_hp()
@@ -467,32 +479,41 @@ def tile_mixtureconfounderprior_pa_s_kernel(
         close_sum(1)
         close_sum(2)
         open_sum(3)
-        close_sum(3)
         normalise(0)
         turn(0)
         take_turned(0)
+        close_sum(3)
         normalise(1)
         turn(1)
         take_turned(1)
         normalise(2)
         turn(2)
         take_turned(2)
-        normalise(3)
+        normalise(3, 0)
         quantise(0)
-        turn(3)
+        normalise(3, 1)
         multiply(0)
+        turn(3)
         take_turned(3)
         quantise(1)
         multiply(1)
         quantise(2)
         multiply(2)
-        add_bias(0)
+        for cols in LEFT, RIGHT:
+            add_bias(0, cols)
+            tanh(0, cols)
+        store(0)
         quantise(3)
         multiply(3)
-        add_bias(1)
-        add_bias(2)
-        for k in range(CODES - 1):
-            finish(k)
-        for first in (0, CF // 2):
-            add_bias(CODES - 1, slice(first, first + CF // 2))
-            finish(CODES - 1, slice(first, first + CF // 2))
+        for cols in LEFT, RIGHT:
+            add_bias(1, cols)
+            tanh(1, cols)
+        store(1)
+        for cols in LEFT, RIGHT:
+            add_bias(2, cols)
+            tanh(2, cols)
+        store(2)
+        for cols in LEFT, RIGHT:
+            add_bias(3, cols)
+            tanh(3, cols)
+            store(3, cols)

from contextlib import ExitStack

import concourse.mybir as mybir
from concourse.masks import make_identity

F32 = mybir.dt.float32
BF16 = mybir.dt.bfloat16
U32 = mybir.dt.uint32
U8 = mybir.dt.uint8
FP8X4 = mybir.dt.float8_e4m3fn_x4
ALU = mybir.AluOpType
ACT = mybir.ActivationFunctionType
AXIS = mybir.AxisListType

P = 128
PACK = 4
D = 1024
PASSES1 = D // (P * PACK)
CODES = 4
CF = 512
CHUNKS = CF // P
HALVES = 2
HALF = CF // HALVES
LEFT, RIGHT = slice(0, HALF), slice(HALF, CF)
REPEATS = 16
LN_EPS = 1e-5

VEC_B1, VEC_G = 4, 5
VECTORS = 6
VEC_ROWS = VECTORS * CHUNKS

W1_VECTOR = 352
W2_VECTOR = 256

FLOPS = 2 * P * D * CF + 2 * P * CODES * CF * CF


def regroup(copy, grouped, rows):
    copy(
        out=grouped.rearrange("p (c i) j -> p c j i", i=4),
        in_=rows.rearrange("p j (c i) -> p c j i", i=4),
    )


def tile_mixtureconfounderprior_pa_s_kernel(
    tc, h, mu_w1_h, code_mu, mu_b1, ln_g, ln_b, mu_w2, mu_b2, out
):
    nc = tc.nc
    h_rows = h.flatten_outer_dims()
    out_rows = out.rearrange("b t k n -> (b t) k n")

    with ExitStack() as stack:
        keep = stack.enter_context(tc.tile_pool(name="keep", bufs=1))
        psum = stack.enter_context(tc.psum_pool(name="psum", bufs=1))
        stack.enter_context(tc.manual_schedule())

        vec_rows = keep.tile([P, P], BF16)
        w1_rows = keep.tile([P, PASSES1, PACK, CF], BF16)
        h_sb = keep.tile([P, D], BF16)
        w2_rows = keep.tile([P, PACK, CF], BF16)
        b_all = keep.tile([P, CF], BF16)
        b2_all = keep.tile([P, CF], BF16)
        ones = keep.tile([P, P], F32)
        table_warm = keep.tile([P, 2], F32)
        ident_bf16 = keep.tile([P, P], BF16)
        ident_f32 = keep.tile([P, P], F32)
        neg_averager = keep.tile([P, P], BF16)
        averager = keep.tile([P, P], F32)
        vec_cols = keep.tile([P, VECTORS, CHUNKS], BF16)
        g_cols = keep.tile([P, CHUNKS], F32)
        neg_g_cols = keep.tile([P, CHUNKS], F32)
        by_code = [P, CODES, CHUNKS]
        by_rep = [P, CODES, REPEATS]
        c_hat_g = keep.tile(by_code, F32)
        c_hat_2 = keep.tile(by_code, F32)
        c_hat_sq = keep.tile(by_code, F32)
        c_sq_sum = keep.tile([P, CODES], F32)
        c_sq_eps = keep.tile([P, CODES], F32)
        h_grouped = keep.tile([P, PASSES1 * P * PACK], BF16, align_bytes=64)
        h_codes = keep.tile([P, PASSES1 * P], U32, align_bytes=64)
        h_scales = keep.tile([P, PASSES1 * P], U8, align_bytes=64)
        w1_grouped = keep.tile([P, PASSES1, CF, PACK], BF16, align_bytes=64)
        w1_codes = keep.tile([P, PASSES1, CF], U32, align_bytes=64)
        w1_scales = keep.tile([P, PASSES1, CF], U8, align_bytes=64)
        w2_grouped = keep.tile([P, CF, PACK], BF16, align_bytes=64)
        w2_codes = keep.tile([P, CF], U32, align_bytes=64)
        w2_scales = keep.tile([P, CF], U8, align_bytes=64)
        unread = keep.tile([P, CF], BF16)
        hp_sum = keep.tile([P, HALVES], F32)
        hp_stats = keep.tile([P, HALVES, 6], F32)
        hp_mean_var = keep.tile([P, 2], F32)
        hpT = keep.tile([P, CHUNKS, P], F32)
        hpT_g = keep.tile([P, CHUNKS, P], F32)
        hpT_hat_g = keep.tile([P, CHUNKS, P], F32)
        rstd = keep.tile([P, CODES], F32)
        mu_ln = keep.tile([P, CODES, CF], BF16)
        ln_grouped = keep.tile([P, CODES, P * PACK], BF16, align_bytes=64)
        ln_codes = keep.tile([P, CODES, P], U32, align_bytes=64)
        ln_scales = keep.tile([P, CODES, P], U8, align_bytes=64)
        result = keep.tile([P, CODES, CF], F32)


        bank = {}

        def open_bank(name, tag, shape, dtype=F32):
            bank[name] = psum.tile(shape, dtype, tag=tag, name=name)
            return bank[name]

        def load_vector(queue, v, rows):
            first = v * CHUNKS
            queue.dma_start(out=vec_rows[first : first + rows.shape[0], :], in_=rows)

        def load_w1(g):
            view = mu_w1_h.rearrange("(g p j) n -> g p j n", g=PASSES1, j=PACK)
            nc.sync.dma_start(out=w1_rows[:, g], in_=view[g])

        def load_w2():
            nc.sync.dma_start(out=w2_rows[:], in_=mu_w2.rearrange("(p j) n -> p j n", j=PACK))

        def keep_warm(times):
            for i in range(times):
                nc.tensor.matmul(bank["idle"][:], ones[:], ones[:], start=True, stop=True)

        def keep_warm2(tag, times):
            for i in range(times):
                nc.tensor.matmul(bank[tag][:, 0:P], ones[:], ones[:], start=True, stop=True)

        def keep_warm_mx(tag, times):
            for i in range(times):
                nc.tensor.matmul_mx(
                    out=bank[tag][:, 0:HALF],
                    lhsT=w1_codes[:, 0, 0:P].bitcast(FP8X4),
                    lhsT_scale=w1_scales[:, 0, 0:P],
                    rhs=w1_codes[:, 0, 0:HALF].bitcast(FP8X4),
                    rhs_scale=w1_scales[:, 0, 0:HALF],
                    start=True,
                    stop=True,
                )

        def turn_h():
            h_words = h_sb[:].bitcast(F32)
            hT_ps = open_bank("hT", "b0", [P, PASSES1, 2, P])
            for g in range(PASSES1):
                for u in range(2):
                    words = slice(2 * P * g + u, 2 * P * (g + 1), 2)
                    nc.tensor.transpose(hT_ps[:, g, u, :], h_words[:, words], ident_f32[:])
            nc.scalar.copy(
                out=h_grouped[:].bitcast(F32).rearrange("p (g t u) -> p g t u", g=PASSES1, u=2),
                in_=hT_ps[:].rearrange("p g u t -> p g t u"),
            )

        def quantise_h():
            nc.vector.quantize_mx(
                out=h_codes[:].bitcast(FP8X4), scales=h_scales[:], in_=h_grouped[:]
            )

        def regroup_w1_vector(g, cols):
            regroup(nc.vector.tensor_copy, w1_grouped[:, g, cols], w1_rows[:, g, :, cols])

        def regroup_w1_scalar(g, cols):
            regroup(nc.scalar.copy, w1_grouped[:, g, cols], w1_rows[:, g, :, cols])

        def quantise_w1(g, cols=slice(0, CF)):
            nc.vector.quantize_mx(
                out=w1_codes[:, g, cols].bitcast(FP8X4),
                scales=w1_scales[:, g, cols],
                in_=w1_grouped[:, g, cols].rearrange("p n j -> p (n j)"),
            )

        def turn_vectors():
            cols_ps = open_bank("cols", "b2", [P, P], BF16)
            nc.tensor.transpose(cols_ps[:], vec_rows[:], ident_bf16[:])

        def take_vectors():
            nc.vector.tensor_copy(
                out=vec_cols[:].rearrange("p v c -> p (v c)"), in_=bank["cols"][:, 0:VEC_ROWS]
            )
            nc.gpsimd.tensor_copy(out=g_cols[:], in_=vec_cols[:, VEC_G, :])
            nc.gpsimd.tensor_scalar(
                out=neg_g_cols[:], in0=g_cols[:], scalar1=-1.0 / CF, scalar2=0.0,
                op0=ALU.mult, op1=ALU.add,
            )

        def centre_codes():
            c_hat_ps = open_bank("c_hat", "b2", by_code)
            codes = vec_cols[:, 0:CODES, :]
            b1 = vec_cols[:, VEC_B1 : VEC_B1 + 1, :]
            terms = [(ident_bf16, codes), (ident_bf16, b1.to_broadcast(by_code))]
            for c in range(CHUNKS):
                terms.append((neg_averager, codes[:, :, c : c + 1].to_broadcast(by_code)))
                terms.append((neg_averager, b1[:, :, c : c + 1].to_broadcast(by_code)))
            for i, (weights, columns) in enumerate(terms):
                nc.tensor.matmul(
                    c_hat_ps[:], weights[:], columns, start=(i == 0), stop=(i == len(terms) - 1)
                )

        def scale_codes():
            nc.vector.tensor_tensor(
                out=c_hat_g[:], in0=bank["c_hat"][:],
                in1=vec_cols[:, VEC_G : VEC_G + 1, :].to_broadcast(by_code), op=ALU.mult,
            )

        def prepare_variances():
            nc.scalar.mul(out=c_hat_2[:], in_=bank["c_hat"][:], mul=2.0 / CF)
            nc.scalar.activation(out=c_hat_sq[:], in_=bank["c_hat"][:], func=ACT.Square)

        def sum_squares():
            nc.vector.tensor_reduce(out=c_sq_sum[:], in_=c_hat_sq[:], axis=AXIS.X, op=ALU.add)

        def add_eps():
            nc.vector.tensor_scalar(
                out=c_sq_eps[:], in0=c_sq_sum[:], scalar1=CHUNKS * LN_EPS, scalar2=None, op0=ALU.add
            )

        def open_sum(k):
            sum_ps = open_bank("sum%d" % k, "b%d" % (4 + k), [P, CF])
            for c in range(CHUNKS):
                nc.tensor.matmul(
                    sum_ps[:, c * P : (c + 1) * P],
                    c_hat_g[:, k, c : c + 1].to_broadcast([P, P]),
                    ident_f32[:],
                    start=(c == 0),
                    stop=False,
                    is_transpose=True,
                )

        def close_sum(k):
            for c in range(CHUNKS):
                nc.tensor.matmul(
                    bank["sum%d" % k][:, c * P : (c + 1) * P],
                    hpT_hat_g[:, c, :],
                    ident_f32[:],
                    start=False,
                    stop=(c == CHUNKS - 1),
                    is_transpose=True,
                )

        def multiply_tokens(half, passes=range(PASSES1)):
            cols = slice(half * HALF, (half + 1) * HALF)
            for g in passes:
                if g == 0:
                    open_bank("hp%d" % half, ("b1", "b7")[half], [P, HALF])
                nc.tensor.matmul_mx(
                    out=bank["hp%d" % half][:],
                    lhsT=h_codes[:, g * P : (g + 1) * P].bitcast(FP8X4),
                    lhsT_scale=h_scales[:, g * P : (g + 1) * P],
                    rhs=w1_codes[:, g, cols].bitcast(FP8X4),
                    rhs_scale=w1_scales[:, g, cols],
                    start=(g == 0),
                    stop=(g == PASSES1 - 1),
                )

        def multiply_features(half):
            if half == 0:
                open_bank("hpT", "b0", [P, CHUNKS, P])
            for c in range(half * CHUNKS // 2, (half + 1) * CHUNKS // 2):
                for g in range(PASSES1):
                    nc.tensor.matmul_mx(
                        out=bank["hpT"][:, c, :],
                        lhsT=w1_codes[:, g, c * P : (c + 1) * P].bitcast(FP8X4),
                        lhsT_scale=w1_scales[:, g, c * P : (c + 1) * P],
                        rhs=h_codes[:, g * P : (g + 1) * P].bitcast(FP8X4),
                        rhs_scale=h_scales[:, g * P : (g + 1) * P],
                        start=(g == 0),
                        stop=(g == PASSES1 - 1),
                    )

        def regroup_w2_scalar():
            regroup(nc.scalar.copy, w2_grouped[:, W2_VECTOR:], w2_rows[:, :, W2_VECTOR:])

        def regroup_w2_vector():
            regroup(nc.vector.tensor_copy, w2_grouped[:, :W2_VECTOR], w2_rows[:, :, :W2_VECTOR])

        def quantise_w2():
            nc.vector.quantize_mx(
                out=w2_codes[:].bitcast(FP8X4),
                scales=w2_scales[:],
                in_=w2_grouped[:].rearrange("p n j -> p (n j)"),
            )

        def sum_hp():
            nc.scalar.activation(
                out=unread[:, 0:HALF], in_=bank["hp0"][:], func=ACT.Identity,
                accum_out=hp_sum[:, 0:1],
            )

        def sum_hp1():
            nc.vector.tensor_reduce(out=hp_sum[:, 1:2], in_=bank["hp1"][:], axis=AXIS.X, op=ALU.add)

        def spread_hp_sum():
            sum_all_ps = open_bank("sum_all", "b2", [P, P])
            for half in range(HALVES):
                nc.tensor.matmul(
                    sum_all_ps[:],
                    hp_sum[:, half : half + 1].to_broadcast([P, P]),
                    ident_f32[:],
                    start=(half == 0),
                    stop=(half == HALVES - 1),
                    is_transpose=True,
                )

        def stats_hp(half):
            nc.vector.bn_stats(out=hp_stats[:, half, :], in_=bank["hp%d" % half][:])

        def aggregate_hp():
            nc.vector.bn_aggr(
                out=hp_mean_var[:], in_=hp_stats[:].rearrange("p h s -> p (h s)")
            )

        def take_features(c):
            nc.scalar.copy(out=hpT[:, c, :], in_=bank["hpT"][:, c, :])

        def scale_features_scalar(c):
            nc.scalar.mul(
                out=hpT_g[:, c, :], in_=bank["hpT"][:, c, :], mul=g_cols[:, c : c + 1]
            )

        def scale_features_vector(c):
            nc.vector.tensor_scalar(
                out=hpT_g[:, c, :], in0=hpT[:, c, :], scalar1=g_cols[:, c : c + 1], scalar2=None,
                op0=ALU.mult,
            )

        def centre_features(c):
            nc.vector.scalar_tensor_tensor(
                out=hpT_hat_g[:, c, :], in0=bank["sum_all"][:], scalar=neg_g_cols[:, c : c + 1],
                in1=hpT_g[:, c, :], op0=ALU.mult, op1=ALU.add,
            )

        def open_variances():
            var_ps = open_bank("var", "b3", by_rep)
            nc.tensor.matmul(
                var_ps[:], averager[:], c_sq_eps[:].unsqueeze(2).to_broadcast(by_rep), start=True, stop=False
            )

        def close_variances(half):
            for c in range(half * CHUNKS // 2, (half + 1) * CHUNKS // 2):
                nc.tensor.matmul(
                    bank["var"][:], hpT[:, c, :], c_hat_2[:, :, c : c + 1].to_broadcast(by_rep),
                    start=False, stop=(c == CHUNKS - 1),
                )

        def take_root():
            nc.scalar.activation(
                out=rstd[:], in_=bank["var"][:, :, 0], func=ACT.Abs_reciprocal_sqrt,
                bias=hp_mean_var[:, 1:2], scale=1.0,
            )

        def normalise(k, parts=None):
            for u in (range(2) if parts is None else (parts,)):
                nc.vector.scalar_tensor_tensor(
                    out=mu_ln[:, k, u * 2 * P : (u + 1) * 2 * P].rearrange("t (p e) -> t p e", e=2),
                    in0=bank["sum%d" % k][:].rearrange("t (p u e) -> t u p e", u=2, e=2)[:, u],
                    scalar=rstd[:, k : k + 1],
                    in1=b_all[:].rearrange("t (p u e) -> t u p e", u=2, e=2)[:, u],
                    op0=ALU.mult, op1=ALU.add,
                )

        def turn(k):
            words = mu_ln[:, k, :].bitcast(F32)
            lnT_ps = open_bank("lnT%d" % k, "b%d" % (4 + k), [P, 2, P])
            for u in range(2):
                nc.tensor.transpose(lnT_ps[:, u, :], words[:, u * P : (u + 1) * P], ident_f32[:])

        def take_turned(k):
            lnT_ps = bank["lnT%d" % k]
            nc.scalar.copy(
                out=ln_grouped[:, k, :].bitcast(F32).rearrange("p (t u) -> p t u", u=2),
                in_=lnT_ps[:].rearrange("p u t -> p t u"),
            )

        def quantise(k):
            nc.vector.quantize_mx(
                out=ln_codes[:, k, :].bitcast(FP8X4),
                scales=ln_scales[:, k, :],
                in_=ln_grouped[:, k, :],
            )

        def multiply(k):
            out_ps = open_bank("out%d" % k, "b%d" % k, [P, CF])
            nc.tensor.matmul_mx(
                out=out_ps[:],
                lhsT=ln_codes[:, k, :].bitcast(FP8X4),
                lhsT_scale=ln_scales[:, k, :],
                rhs=w2_codes[:].bitcast(FP8X4),
                rhs_scale=w2_scales[:],
                start=True,
                stop=True,
            )

        def add_bias(k, cols=slice(0, CF)):
            nc.vector.tensor_tensor(
                out=result[:, k, cols], in0=bank["out%d" % k][:, cols], in1=b2_all[:, cols],
                op=ALU.add,
            )

        def tanh(k, cols=slice(0, CF)):
            nc.scalar.activation(out=result[:, k, cols], in_=result[:, k, cols], func=ACT.Tanh)

        def store(k, cols=slice(0, CF)):
            nc.sync.dma_start(out=out_rows[:, k, cols], in_=result[:, k, cols])

        code_rows = code_mu.rearrange("k (c p) -> (k c) p", p=P)
        load_vector(nc.scalar, 0, code_rows)
        load_vector(nc.scalar, VEC_B1, mu_b1.rearrange("(c p) -> c p", p=P))
        load_vector(nc.sync, VEC_G, ln_g.rearrange("(c p) -> c p", p=P))
        load_vector(nc.sync, VECTORS, code_rows[0 : 32 - VEC_ROWS, :])
        nc.vector.memset(ones[:], 1.0)
        nc.vector.memset(vec_rows[32:64, :], 0.0)
        nc.vector.memset(vec_rows[64:128, :], 0.0)
        load_w1(0)
        nc.sync.dma_start(out=h_sb[:], in_=h_rows)
        load_w1(1)
        load_w2()
        nc.sync.dma_start(out=b_all[:], in_=ln_b.partition_broadcast(P))
        nc.sync.dma_start(out=b2_all[:], in_=mu_b2.partition_broadcast(P))

        nc.scalar.activation(
            out=table_warm[:, 0:1], in_=ones[:, 0:1], func=ACT.Abs_reciprocal_sqrt
        )
        make_identity(nc, ident_bf16[:])
        make_identity(nc, ident_f32[:])
        nc.gpsimd.memset(neg_averager[:], -1.0 / CF)
        nc.gpsimd.memset(averager[:], 1.0 / CF)
        open_bank("idle", "b3", [P, P])
        keep_warm(3)
        turn_vectors()
        take_vectors()
        keep_warm(1)
        centre_codes()
        regroup_w1_vector(0, LEFT)
        regroup_w1_vector(0, slice(HALF, W1_VECTOR))
        regroup_w1_scalar(0, slice(W1_VECTOR, CF))
        scale_codes()
        prepare_variances()
        quantise_w1(0, LEFT)
        quantise_w1(0, RIGHT)
        sum_squares()
        keep_warm(1)
        turn_h()
        open_sum(0)
        open_sum(1)
        open_sum(2)
        regroup_w1_vector(1, slice(0, W1_VECTOR))
        regroup_w1_scalar(1, slice(W1_VECTOR, CF))
        add_eps()
        quantise_h()
        quantise_w1(1, LEFT)
        quantise_w1(1, RIGHT)
        open_variances()
        multiply_tokens(0)
        multiply_tokens(1)
        multiply_features(0)
        multiply_features(1)

        regroup_w2_scalar()
        regroup_w2_vector()
        sum_hp()
        sum_hp1()
        stats_hp(1)
        spread_hp_sum()
        for c in range(CHUNKS):
            take_features(c)
        close_variances(0)
        close_variances(1)
        for c in range(CHUNKS):
            if c < CHUNKS // 2:
                scale_features_vector(c)
            else:
                scale_features_scalar(c)
        stats_hp(0)
        for c in range(CHUNKS):
            centre_features(c)
        aggregate_hp()
        take_root()
        nc.scalar.activation(out=table_warm[:, 1:2], in_=rstd[:, 0:1], func=ACT.Tanh)
        quantise_w2()
        close_sum(0)
        close_sum(1)
        close_sum(2)
        open_sum(3)
        normalise(0)
        turn(0)
        take_turned(0)
        close_sum(3)
        normalise(1)
        turn(1)
        take_turned(1)
        normalise(2)
        turn(2)
        take_turned(2)
        normalise(3, 0)
        quantise(0)
        normalise(3, 1)
        multiply(0)
        turn(3)
        take_turned(3)
        quantise(1)
        multiply(1)
        quantise(2)
        multiply(2)
        for cols in LEFT, RIGHT:
            add_bias(0, cols)
            tanh(0, cols)
        store(0)
        quantise(3)
        multiply(3)
        for cols in LEFT, RIGHT:
            add_bias(1, cols)
            tanh(1, cols)
        store(1)
        for cols in LEFT, RIGHT:
            add_bias(2, cols)
            tanh(2, cols)
        store(2)
        for cols in LEFT, RIGHT:
            add_bias(3, cols)
            tanh(3, cols)
            store(3, cols)
